import numpy as np
import ml_dtypes


def mxq(x, axis, fmt="e4m3"):
    dtype, down = {"e4m3": (ml_dtypes.float8_e4m3fn, 7), "e5m2": (ml_dtypes.float8_e5m2, 14)}[fmt]
    v = np.moveaxis(np.asarray(x, np.float32).astype(ml_dtypes.bfloat16).astype(np.float64), axis, -1)
    blocks = v.reshape(v.shape[:-1] + (-1, 32))
    amax = np.abs(blocks).max(-1, keepdims=True)
    byte = np.maximum(np.where(amax > 0, np.frexp(amax)[1] - 1 + 127, 0) - down, 1)
    scale = np.exp2(byte - 127.0)
    codes = (blocks / scale).astype(np.float32).astype(dtype).astype(np.float64)
    return np.moveaxis((codes * scale).reshape(v.shape), -1, axis)


WIDE = False


def mx_kscale(k):
    if not WIDE:
        return np.ones(k)
    levels = np.array([10, -10, 5, -5, 0])
    if k % 512:
        return np.exp2(np.random.permutation(np.resize(levels, k // 32))).repeat(32)
    a = np.empty((k // 512, 16))
    for p in range(k // 512):
        a[p, :8] = np.random.permutation(np.resize(levels, 8))
        for g in range(8):
            far = levels[np.abs(levels - a[p, g]) >= 10]
            a[p, g + 8] = far[np.random.randint(len(far))]
    return np.exp2(a.ravel()).repeat(32)


BF16 = ml_dtypes.bfloat16


def bf(x):
    return np.asarray(x, np.float32).astype(BF16)


def f64(x):
    return np.asarray(x).astype(np.float64)


B, H, T, N, D, GRID = 1, 4, 512, 2048, 256, 32


def rot_pairs(v):
    return np.stack((-v[..., 1::2], v[..., ::2]), axis=-1).reshape(v.shape)


def rope(v, c, s):
    return v * c + rot_pairs(v) * s


def setup_inputs():
    s = np.repeat(mx_kscale(N)[::2], 2)
    t = mx_kscale(T)
    u = np.random.random((T, N))
    return {"Q": bf(np.random.standard_normal((B, H, T, N)) * s),
            "K": bf(np.random.standard_normal((B, H, T, N)) * t[:, None] / s),
            "V": bf(np.random.standard_normal((B, 1, T, D)) * 2.0 / np.sqrt(T) / t[:, None]),
            "cos_t": bf(np.cos(2.0 * np.pi * u)),
            "sin_t": bf(np.sin(2.0 * np.pi * u))}


def reference(Q, K, V, cos_t, sin_t):
    c, s = f64(cos_t), f64(sin_t)
    qr = rope(f64(Q), c, s)
    kr = rope(f64(K), c, s)
    scores = (mxq(qr, 3, "e4m3") @ mxq(kr, 3, "e4m3").transpose(0, 1, 3, 2)) / np.sqrt(N)
    return mxq(scores, 3, "e4m3") @ mxq(f64(V), 2, "e4m3")

@@ -1,0 +1,311 @@
+from contextlib import ExitStack
+
+import concourse.mybir as mybir
+from concourse.masks import make_identity
+
+F32 = mybir.dt.float32
+BF16 = mybir.dt.bfloat16
+U32 = mybir.dt.uint32
+U8 = mybir.dt.uint8
+FP8X4 = mybir.dt.float8_e4m3fn_x4
+MULT = mybir.AluOpType.mult
+COPY = mybir.ActivationFunctionType.Copy
+
+P = 128
+H = 4
+T = 512
+N = 2048
+D = 256
+TT = T // P
+NG = N // 512
+NI = N // 2
+NB = 384
+NBB = NB // P
+NTB = 8 + NBB
+AHEAD = 3
+FLOPS = 2 * H * T * T * N + 2 * H * T * T * D
+
+
+def tile_bidirectionalattention_pa_kernel(tc, Q, K, V, cos_t, sin_t, out):
+    nc = tc.nc
+    Qr = Q.flatten_outer_dims().rearrange("(h p j) n -> h j p n", p=P, j=TT)
+    Kr = K.flatten_outer_dims().rearrange("(h p j) n -> h j p n", p=P, j=TT)
+    Vf = V.flatten_outer_dims()
+    outr = out.flatten_outer_dims().rearrange("(h p j) d -> h j p d", p=P, j=TT)
+    cosr = cos_t.rearrange("(p j) n -> j p n", j=TT)
+    sinr = sin_t.rearrange("(p j) n -> j p n", j=TT)
+    inv_sqrt_n = 1.0 / (float(N) ** 0.5)
+
+    with ExitStack() as ctx:
+        const = ctx.enter_context(tc.tile_pool(name="const", bufs=1))
+        xpool = ctx.enter_context(tc.tile_pool(name="xpool", bufs=AHEAD + 1))
+        prod = ctx.enter_context(tc.tile_pool(name="prod", bufs=3))
+        gpool = ctx.enter_context(tc.tile_pool(name="gpool", bufs=3))
+        qpool = ctx.enter_context(tc.tile_pool(name="qpool", bufs=2))
+        spool = ctx.enter_context(tc.tile_pool(name="spool", bufs=2))
+        tabp = ctx.enter_context(tc.psum_pool(name="tabp", bufs=1))
+        accp = ctx.enter_context(tc.psum_pool(name="accp", bufs=3))
+        scp = ctx.enter_context(tc.psum_pool(name="scp", bufs=1))
+        op = ctx.enter_context(tc.psum_pool(name="op", bufs=1))
+        ctx.enter_context(tc.manual_schedule())
+
+        ident = const.tile([P, P], F32, name="ident")
+        make_identity(nc, ident[:])
+
+        cos_sb = []
+        sin_sb = []
+        sneg = []
+        tab_t = []
+        for tau in range(TT):
+            cos_sb.append(const.tile([P, N], BF16, name="cos%d" % tau))
+            sin_sb.append(const.tile([P, N], BF16, name="sin%d" % tau))
+            sneg.append(const.tile([P, NI - NB], BF16, name="sneg%d" % tau))
+            tab_t.append(const.tile([P, NTB, P], F32, name="tabt%d" % tau))
+        kcodes = const.tile([P, H * TT, 512], U32, name="kcodes", align_bytes=64)
+        kscales = const.tile([P, H * TT, 512], U8, name="kscales", align_bytes=64)
+        v_raw = const.tile([P, 4, D], BF16, name="v_raw")
+        v_grp = const.tile([P, D, 4], BF16, name="v_grp", align_bytes=64)
+        vcodes = const.tile([P, D], U32, name="vcodes", align_bytes=64)
+        vscales = const.tile([P, D], U8, name="vscales", align_bytes=64)
+
+        units = []
+        for which in range(2):
+            for tau in range(TT):
+                for h in range(H):
+                    units.append((which, tau, h))
+        NU = len(units)
+        state = {}
+
+        def load_tables(tau):
+            nc.sync.dma_start(out=cos_sb[tau][:], in_=cosr[tau, :, :])
+            nc.sync.dma_start(out=sin_sb[tau][:], in_=sinr[tau, :, :])
+
+        def load(u):
+            which, tau, h = units[u]
+            src = Kr if which == 0 else Qr
+            x = xpool.tile([P, N], BF16, name="x")
+            nc.sync.dma_start(out=x[:], in_=src[h, tau, :, :])
+            state[("x", u)] = x
+
+        def negate_sin(tau):
+            sv = sin_sb[tau][:].rearrange("p (i e) -> p e i", e=2)
+            nc.scalar.mul(out=sneg[tau][:], in_=sv[:, 0, NB:NI], mul=-1.0)
+
+        def tables_flip(tau):
+            cw = cos_sb[tau][:].bitcast(F32)
+            sw = sin_sb[tau][:].bitcast(F32)
+            for b0 in range(0, NTB, 4):
+                n = min(4, NTB - b0)
+                ps = accp.tile([P, 4, P], F32, name="ps")
+                for k in range(n):
+                    b = b0 + k
+                    srcw = cw[:, b * P : (b + 1) * P] if b < 8 else sw[:, (b - 8) * P : (b - 7) * P]
+                    nc.tensor.transpose(ps[:, k, :], srcw, ident[:])
+                nc.scalar.copy(out=tab_t[tau][:, b0 : b0 + n, :], in_=ps[:, 0:n, :])
+
+        def tables_back(tau, part):
+            if part == 0:
+                t = tabp.tile([P, 512], F32, name="tabc0")
+                blocks = range(0, 4)
+            elif part == 1:
+                t = tabp.tile([P, 512], F32, name="tabc1")
+                blocks = range(4, 8)
+            else:
+                t = tabp.tile([P, 512], F32, name="tabs")
+                blocks = range(8, NTB)
+            for k, b in enumerate(blocks):
+                nc.tensor.transpose(t[:, k * P : (k + 1) * P], tab_t[tau][:, b, :], ident[:])
+            state[("tab", part)] = t
+
+        def pair_view(ap):
+            return ap.rearrange("p (i e) -> p e i", e=2)
+
+        def products_begin(u):
+            a = prod.tile([P, 2, NI], F32, name="a")
+            b = prod.tile([P, 2, NI], F32, name="b")
+            state[("ab", u)] = (a, b)
+
+        def product_cos(u, part):
+            which, tau, h = units[u]
+            xv = pair_view(state[("x", u)][:])
+            a, b = state[("ab", u)]
+            rng = slice(part * 512, (part + 1) * 512)
+            if u == 0:
+                cv = pair_view(cos_sb[tau][:])[:, :, rng]
+            else:
+                cv = pair_view(state[("tab", part)][:].bitcast(BF16))
+            nc.vector.tensor_tensor(out=a[:, :, rng], in0=xv[:, :, rng], in1=cv, op=MULT)
+
+        def product_sin_vector(u):
+            which, tau, h = units[u]
+            xv = pair_view(state[("x", u)][:])
+            a, b = state[("ab", u)]
+            if u == 0:
+                sv = pair_view(sin_sb[tau][:])[:, :, 0:NB]
+            else:
+                sv = pair_view(state[("tab", 2)][:].bitcast(BF16)[:, 0 : 2 * NB])
+            nc.vector.scalar_tensor_tensor(
+                out=b[:, 0, 0:NB], in0=xv[:, 1, 0:NB], scalar=-1.0, in1=sv[:, 0, :], op0=MULT, op1=MULT
+            )
+            nc.vector.tensor_tensor(out=b[:, 1, 0:NB], in0=xv[:, 0, 0:NB], in1=sv[:, 1, :], op=MULT)
+
+        def product_sin_gpsimd(u):
+            which, tau, h = units[u]
+            xv = pair_view(state[("x", u)][:])
+            sv = pair_view(sin_sb[tau][:])
+            a, b = state[("ab", u)]
+            nc.gpsimd.tensor_tensor(out=b[:, 0, NB:NI], in0=xv[:, 1, NB:NI], in1=sneg[tau][:], op=MULT)
+            nc.gpsimd.tensor_tensor(out=b[:, 1, NB:NI], in0=xv[:, 0, NB:NI], in1=sv[:, 1, NB:NI], op=MULT)
+
+        def rotate_sum(u):
+            a, b = state[("ab", u)]
+            grp = gpool.tile([P, NG, P, 4], BF16, name="grp", align_bytes=64)
+            for g in range(NG):
+                ps = accp.tile([P, 4, P], F32, name="ps")
+                for half in range(2):
+                    for e in range(2):
+                        cols = slice(256 * g + half, 256 * (g + 1), 2)
+                        dst = ps[:, 2 * half + e, :]
+                        nc.tensor.matmul(
+                            out=dst, lhsT=a[:, e, cols], rhs=ident[:], start=True, stop=False, is_transpose=True
+                        )
+                        nc.tensor.matmul(
+                            out=dst, lhsT=b[:, e, cols], rhs=ident[:], start=False, stop=True, is_transpose=True
+                        )
+                nc.scalar.copy(out=grp[:, g, :, :], in_=ps[:].rearrange("p j t -> p t j"))
+            state[("grp", u)] = grp
+
+        def quantise(u):
+            which, tau, h = units[u]
+            grp = state[("grp", u)]
+            if which == 0:
+                codes = kcodes[:, h * TT + tau, :]
+                scales = kscales[:, h * TT + tau, :]
+            else:
+                qc = qpool.tile([P, 512], U32, name="qc", align_bytes=64)
+                qs = qpool.tile([P, 512], U8, name="qs", align_bytes=64)
+                codes = qc[:]
+                scales = qs[:]
+                state[("q", u)] = (qc, qs)
+            nc.vector.quantize_mx(
+                out=codes.bitcast(FP8X4), scales=scales, in_=grp[:].rearrange("p g t j -> p (g t j)")
+            )
+
+        def scores(u):
+            which, tau, h = units[u]
+            qc, qs = state[("q", u)]
+            sc = scp.tile([P, TT, P], F32, name="sc")
+            for tk in range(TT):
+                for g in range(NG):
+                    cols = slice(g * P, (g + 1) * P)
+                    nc.tensor.matmul_mx(
+                        out=sc[:, tk, :],
+                        lhsT=kcodes[:, h * TT + tk, cols].bitcast(FP8X4),
+                        lhsT_scale=kscales[:, h * TT + tk, cols],
+                        rhs=qc[:, cols].bitcast(FP8X4),
+                        rhs_scale=qs[:, cols],
+                        start=(g == 0),
+                        stop=(g == NG - 1),
+                    )
+            state[("sc", u)] = sc
+
+        def scores_out(u):
+            sc = state[("sc", u)]
+            sg = spool.tile([P, P, 4], BF16, name="sg", align_bytes=64)
+            nc.scalar.activation(out=sg[:], in_=sc[:].rearrange("p j q -> p q j"), func=COPY, scale=inv_sqrt_n)
+            state[("sg", u)] = sg
+
+        def scores_quantise(u):
+            sg = state[("sg", u)]
+            scd = spool.tile([P, P], U32, name="scd", align_bytes=64)
+            ssc = spool.tile([P, P], U8, name="ssc", align_bytes=64)
+            nc.vector.quantize_mx(out=scd[:].bitcast(FP8X4), scales=ssc[:], in_=sg[:].rearrange("p q j -> p (q j)"))
+            state[("scd", u)] = (scd, ssc)
+
+        def values(u):
+            scd, ssc = state[("scd", u)]
+            o_ps = op.tile([P, D], F32, name="o_ps")
+            nc.tensor.matmul_mx(
+                out=o_ps[:],
+                lhsT=scd[:].bitcast(FP8X4),
+                lhsT_scale=ssc[:],
+                rhs=vcodes[:].bitcast(FP8X4),
+                rhs_scale=vscales[:],
+                start=True,
+                stop=True,
+            )
+            state[("o", u)] = o_ps
+
+        def store(u):
+            which, tau, h = units[u]
+            o_ps = state[("o", u)]
+            o_sb = spool.tile([P, D], F32, name="o_sb")
+            nc.scalar.copy(out=o_sb[:], in_=o_ps[:])
+            nc.sync.dma_start(out=outr[h, tau, :, :], in_=o_sb[:])
+
+        def is_q(u):
+            return 0 <= u < NU and units[u][0] == 1
+
+        nc.sync.dma_start(out=cos_sb[0][:], in_=cosr[0, :, :])
+        load(0)
+        nc.sync.dma_start(out=sin_sb[0][:], in_=sinr[0, :, :])
+        for u in range(1, AHEAD):
+            load(u)
+        nc.scalar.dma_start(out=v_raw[:], in_=Vf.rearrange("(p j) d -> p j d", j=TT))
+        nc.scalar.copy(out=v_grp[:], in_=v_raw[:].rearrange("p j d -> p d j"))
+        nc.vector.quantize_mx(
+            out=vcodes[:].bitcast(FP8X4), scales=vscales[:], in_=v_grp[:].rearrange("p d j -> p (d j)")
+        )
+        idle = scp.tile([P, TT, P], F32, name="sc")
+        negate_sin(0)
+        tables_flip(0)
+        for part in range(3):
+            tables_back(0, part)
+
+        for s in range(NU + 4):
+            if s < NU and units[s][0] == 0 and units[s][2] == 0 and units[s][1] + 1 < TT:
+                load_tables(units[s][1] + 1)
+            if s + AHEAD < NU:
+                load(s + AHEAD)
+            last_of_phase = s < NU - 1 and units[s][2] == H - 1
+            next_tau = units[s + 1][1] if s < NU - 1 else 0
+            if 0 <= s - 2 < NU:
+                quantise(s - 2)
+            if s < NU:
+                products_begin(s)
+                product_sin_gpsimd(s)
+                product_cos(s, 0)
+            if is_q(s - 3):
+                scores_quantise(s - 3)
+            if s < NU:
+                product_cos(s, 1)
+                product_sin_vector(s)
+            if s < NU and units[s][0] == 0 and units[s][2] == 2 and units[s][1] + 1 < TT:
+                negate_sin(units[s][1] + 1)
+                tables_flip(units[s][1] + 1)
+            if 0 <= s - 1 < NU:
+                rotate_sum(s - 1)
+            if last_of_phase:
+                tables_back(next_tau, 0)
+                tables_back(next_tau, 1)
+            if is_q(s - 2):
+                scores(s - 2)
+            elif 0 <= s - 1 < NU:
+                for k in range(16):
+                    nc.tensor.matmul_mx(
+                        out=idle[:, k % 4, :],
+                        lhsT=vcodes[:, 0:P].bitcast(FP8X4),
+                        lhsT_scale=vscales[:, 0:P],
+                        rhs=vcodes[:, P : 2 * P].bitcast(FP8X4),
+                        rhs_scale=vscales[:, P : 2 * P],
+                        start=True,
+                        stop=True,
+                    )
+            if is_q(s - 3):
+                values(s - 3)
+            if last_of_phase:
+                tables_back(next_tau, 2)
+            if is_q(s - 2):
+                scores_out(s - 2)
+            if is_q(s - 3):
+                store(s - 3)

@@ -18,10 +18,10 @@ N = 2048
 D = 256
 TT = T // P
 NG = N // 512
-NI = N // 2
-NB = 384
-NBB = NB // P
-NTB = 8 + NBB
+NQ = N // 4
+QV = 384
+NSV = 2 * QV // 2 // P
+NTB = 8 + NSV
 AHEAD = 3
 FLOPS = 2 * H * T * T * N + 2 * H * T * T * D
 
@@ -55,11 +55,13 @@ def tile_bidirectionalattention_pa_kernel(tc, Q, K, V, cos_t, sin_t, out):
         cos_sb = []
         sin_sb = []
         sneg = []
+        sodd = []
         tab_t = []
         for tau in range(TT):
             cos_sb.append(const.tile([P, N], BF16, name="cos%d" % tau))
             sin_sb.append(const.tile([P, N], BF16, name="sin%d" % tau))
-            sneg.append(const.tile([P, NI - NB], BF16, name="sneg%d" % tau))
+            sneg.append(const.tile([P, 2, NQ], BF16, name="sneg%d" % tau))
+            sodd.append(const.tile([P, 2, QV], BF16, name="sodd%d" % tau))
             tab_t.append(const.tile([P, NTB, P], F32, name="tabt%d" % tau))
         kcodes = const.tile([P, H * TT, 512], U32, name="kcodes", align_bytes=64)
         kscales = const.tile([P, H * TT, 512], U8, name="kscales", align_bytes=64)
@@ -87,13 +89,17 @@ def tile_bidirectionalattention_pa_kernel(tc, Q, K, V, cos_t, sin_t, out):
             nc.sync.dma_start(out=x[:], in_=src[h, tau, :, :])
             state[("x", u)] = x
 
-        def negate_sin(tau):
-            sv = sin_sb[tau][:].rearrange("p (i e) -> p e i", e=2)
-            nc.scalar.mul(out=sneg[tau][:], in_=sv[:, 0, NB:NI], mul=-1.0)
+        def quad_view(ap):
+            return ap.rearrange("p (q j) -> p j q", j=4)
+
+        def arrange_sin(tau):
+            sv = quad_view(sin_sb[tau][:])
+            nc.scalar.mul(out=sneg[tau][:], in_=sv[:, 0:4:2, :], mul=-1.0)
+            nc.scalar.copy(out=sodd[tau][:], in_=sv[:, 1:4:2, 0:QV])
 
         def tables_flip(tau):
             cw = cos_sb[tau][:].bitcast(F32)
-            sw = sin_sb[tau][:].bitcast(F32)
+            sw = sodd[tau][:].rearrange("p u q -> p (u q)").bitcast(F32)
             for b0 in range(0, NTB, 4):
                 n = min(4, NTB - b0)
                 ps = accp.tile([P, 4, P], F32, name="ps")
@@ -117,61 +123,56 @@ def tile_bidirectionalattention_pa_kernel(tc, Q, K, V, cos_t, sin_t, out):
                 nc.tensor.transpose(t[:, k * P : (k + 1) * P], tab_t[tau][:, b, :], ident[:])
             state[("tab", part)] = t
 
-        def pair_view(ap):
-            return ap.rearrange("p (i e) -> p e i", e=2)
-
         def products_begin(u):
-            a = prod.tile([P, 2, NI], F32, name="a")
-            b = prod.tile([P, 2, NI], F32, name="b")
+            a = prod.tile([P, 4, NQ], F32, name="a")
+            b = prod.tile([P, 4, NQ], F32, name="b")
             state[("ab", u)] = (a, b)
 
         def product_cos(u, part):
             which, tau, h = units[u]
-            xv = pair_view(state[("x", u)][:])
+            xv = quad_view(state[("x", u)][:])
             a, b = state[("ab", u)]
-            rng = slice(part * 512, (part + 1) * 512)
+            rng = slice(part * 256, (part + 1) * 256)
             if u == 0:
-                cv = pair_view(cos_sb[tau][:])[:, :, rng]
+                cv = quad_view(cos_sb[tau][:])[:, :, rng]
             else:
-                cv = pair_view(state[("tab", part)][:].bitcast(BF16))
+                cv = quad_view(state[("tab", part)][:].bitcast(BF16))
             nc.vector.tensor_tensor(out=a[:, :, rng], in0=xv[:, :, rng], in1=cv, op=MULT)
 
         def product_sin_vector(u):
             which, tau, h = units[u]
-            xv = pair_view(state[("x", u)][:])
+            xv = quad_view(state[("x", u)][:])
             a, b = state[("ab", u)]
             if u == 0:
-                sv = pair_view(sin_sb[tau][:])[:, :, 0:NB]
+                sv = sodd[tau][:]
             else:
-                sv = pair_view(state[("tab", 2)][:].bitcast(BF16)[:, 0 : 2 * NB])
-            nc.vector.scalar_tensor_tensor(
-                out=b[:, 0, 0:NB], in0=xv[:, 1, 0:NB], scalar=-1.0, in1=sv[:, 0, :], op0=MULT, op1=MULT
-            )
-            nc.vector.tensor_tensor(out=b[:, 1, 0:NB], in0=xv[:, 0, 0:NB], in1=sv[:, 1, :], op=MULT)
+                sv = state[("tab", 2)][:].bitcast(BF16)[:, 0 : 2 * QV].rearrange("p (u q) -> p u q", u=2)
+            nc.vector.tensor_tensor(out=b[:, 1:4:2, 0:QV], in0=xv[:, 0:4:2, 0:QV], in1=sv, op=MULT)
 
         def product_sin_gpsimd(u):
             which, tau, h = units[u]
-            xv = pair_view(state[("x", u)][:])
-            sv = pair_view(sin_sb[tau][:])
+            xv = quad_view(state[("x", u)][:])
+            sv = quad_view(sin_sb[tau][:])
             a, b = state[("ab", u)]
-            nc.gpsimd.tensor_tensor(out=b[:, 0, NB:NI], in0=xv[:, 1, NB:NI], in1=sneg[tau][:], op=MULT)
-            nc.gpsimd.tensor_tensor(out=b[:, 1, NB:NI], in0=xv[:, 0, NB:NI], in1=sv[:, 1, NB:NI], op=MULT)
+            nc.gpsimd.tensor_tensor(out=b[:, 0:4:2, :], in0=xv[:, 1:4:2, :], in1=sneg[tau][:], op=MULT)
+            nc.gpsimd.tensor_tensor(
+                out=b[:, 1:4:2, QV:NQ], in0=xv[:, 0:4:2, QV:NQ], in1=sv[:, 1:4:2, QV:NQ], op=MULT
+            )
 
         def rotate_sum(u):
             a, b = state[("ab", u)]
             grp = gpool.tile([P, NG, P, 4], BF16, name="grp", align_bytes=64)
             for g in range(NG):
                 ps = accp.tile([P, 4, P], F32, name="ps")
-                for half in range(2):
-                    for e in range(2):
-                        cols = slice(256 * g + half, 256 * (g + 1), 2)
-                        dst = ps[:, 2 * half + e, :]
-                        nc.tensor.matmul(
-                            out=dst, lhsT=a[:, e, cols], rhs=ident[:], start=True, stop=False, is_transpose=True
-                        )
-                        nc.tensor.matmul(
-                            out=dst, lhsT=b[:, e, cols], rhs=ident[:], start=False, stop=True, is_transpose=True
-                        )
+                cols = slice(g * P, (g + 1) * P)
+                for j in range(4):
+                    dst = ps[:, j, :]
+                    nc.tensor.matmul(
+                        out=dst, lhsT=a[:, j, cols], rhs=ident[:], start=True, stop=False, is_transpose=True
+                    )
+                    nc.tensor.matmul(
+                        out=dst, lhsT=b[:, j, cols], rhs=ident[:], start=False, stop=True, is_transpose=True
+                    )
                 nc.scalar.copy(out=grp[:, g, :, :], in_=ps[:].rearrange("p j t -> p t j"))
             state[("grp", u)] = grp
 
@@ -256,8 +257,7 @@ def tile_bidirectionalattention_pa_kernel(tc, Q, K, V, cos_t, sin_t, out):
         nc.vector.quantize_mx(
             out=vcodes[:].bitcast(FP8X4), scales=vscales[:], in_=v_grp[:].rearrange("p d j -> p (d j)")
         )
-        idle = scp.tile([P, TT, P], F32, name="sc")
-        negate_sin(0)
+        arrange_sin(0)
         tables_flip(0)
         for part in range(3):
             tables_back(0, part)
@@ -281,7 +281,7 @@ def tile_bidirectionalattention_pa_kernel(tc, Q, K, V, cos_t, sin_t, out):
                 product_cos(s, 1)
                 product_sin_vector(s)
             if s < NU and units[s][0] == 0 and units[s][2] == 2 and units[s][1] + 1 < TT:
-                negate_sin(units[s][1] + 1)
+                arrange_sin(units[s][1] + 1)
                 tables_flip(units[s][1] + 1)
             if 0 <= s - 1 < NU:
                 rotate_sum(s - 1)
@@ -290,17 +290,6 @@ def tile_bidirectionalattention_pa_kernel(tc, Q, K, V, cos_t, sin_t, out):
                 tables_back(next_tau, 1)
             if is_q(s - 2):
                 scores(s - 2)
-            elif 0 <= s - 1 < NU:
-                for k in range(16):
-                    nc.tensor.matmul_mx(
-                        out=idle[:, k % 4, :],
-                        lhsT=vcodes[:, 0:P].bitcast(FP8X4),
-                        lhsT_scale=vscales[:, 0:P],
-                        rhs=vcodes[:, P : 2 * P].bitcast(FP8X4),
-                        rhs_scale=vscales[:, P : 2 * P],
-                        start=True,
-                        stop=True,
-                    )
             if is_q(s - 3):
                 values(s - 3)
             if last_of_phase:

@@ -40,7 +40,7 @@ def tile_bidirectionalattention_pa_kernel(tc, Q, K, V, cos_t, sin_t, out):
         const = ctx.enter_context(tc.tile_pool(name="const", bufs=1))
         xpool = ctx.enter_context(tc.tile_pool(name="xpool", bufs=AHEAD + 1))
         prod = ctx.enter_context(tc.tile_pool(name="prod", bufs=3))
-        gpool = ctx.enter_context(tc.tile_pool(name="gpool", bufs=3))
+        shared = ctx.enter_context(tc.tile_pool(name="shared", bufs=1))
         qpool = ctx.enter_context(tc.tile_pool(name="qpool", bufs=2))
         spool = ctx.enter_context(tc.tile_pool(name="spool", bufs=2))
         tabp = ctx.enter_context(tc.psum_pool(name="tabp", bufs=1))
@@ -125,7 +125,8 @@ def tile_bidirectionalattention_pa_kernel(tc, Q, K, V, cos_t, sin_t, out):
 
         def products_begin(u):
             a = prod.tile([P, 4, NQ], F32, name="a")
-            b = prod.tile([P, 4, NQ], F32, name="b")
+            k = u % 3
+            b = shared.tile([P, 4, NQ], F32, name="b%d" % k, offset=k * 16 * NQ, align_bytes=64)
             state[("ab", u)] = (a, b)
 
         def product_cos(u, part):
@@ -161,7 +162,8 @@ def tile_bidirectionalattention_pa_kernel(tc, Q, K, V, cos_t, sin_t, out):
 
         def rotate_sum(u):
             a, b = state[("ab", u)]
-            grp = gpool.tile([P, NG, P, 4], BF16, name="grp", align_bytes=64)
+            k = (u + 2) % 3
+            grp = shared.tile([P, NG, P, 4], BF16, name="g%d" % k, offset=k * 16 * NQ, align_bytes=64)
             for g in range(NG):
                 ps = accp.tile([P, 4, P], F32, name="ps")
                 cols = slice(g * P, (g + 1) * P)
@@ -262,7 +264,7 @@ def tile_bidirectionalattention_pa_kernel(tc, Q, K, V, cos_t, sin_t, out):
         for part in range(3):
             tables_back(0, part)
 
-        for s in range(NU + 4):
+        for s in range(NU + 5):
             if s < NU and units[s][0] == 0 and units[s][2] == 0 and units[s][1] + 1 < TT:
                 load_tables(units[s][1] + 1)
             if s + AHEAD < NU:
@@ -271,12 +273,12 @@ def tile_bidirectionalattention_pa_kernel(tc, Q, K, V, cos_t, sin_t, out):
             next_tau = units[s + 1][1] if s < NU - 1 else 0
             if 0 <= s - 2 < NU:
                 quantise(s - 2)
+            if is_q(s - 4):
+                scores_quantise(s - 4)
             if s < NU:
                 products_begin(s)
                 product_sin_gpsimd(s)
                 product_cos(s, 0)
-            if is_q(s - 3):
-                scores_quantise(s - 3)
             if s < NU:
                 product_cos(s, 1)
                 product_sin_vector(s)
@@ -290,11 +292,11 @@ def tile_bidirectionalattention_pa_kernel(tc, Q, K, V, cos_t, sin_t, out):
                 tables_back(next_tau, 1)
             if is_q(s - 2):
                 scores(s - 2)
-            if is_q(s - 3):
-                values(s - 3)
+            if is_q(s - 4):
+                values(s - 4)
             if last_of_phase:
                 tables_back(next_tau, 2)
             if is_q(s - 2):
                 scores_out(s - 2)
-            if is_q(s - 3):
-                store(s - 3)
+            if is_q(s - 4):
+                store(s - 4)

@@ -19,10 +19,11 @@ D = 256
 TT = T // P
 NG = N // 512
 NQ = N // 4
-QV = 384
-NSV = 2 * QV // 2 // P
-NTB = 8 + NSV
+QV = 208
 AHEAD = 3
+SLOTS = 4
+QUANT = 3
+FINISH = 5
 FLOPS = 2 * H * T * T * N + 2 * H * T * T * D
 
 
@@ -31,56 +32,62 @@ def tile_bidirectionalattention_pa_kernel(tc, Q, K, V, cos_t, sin_t, out):
     Qr = Q.flatten_outer_dims().rearrange("(h p j) n -> h j p n", p=P, j=TT)
     Kr = K.flatten_outer_dims().rearrange("(h p j) n -> h j p n", p=P, j=TT)
     Vf = V.flatten_outer_dims()
-    outr = out.flatten_outer_dims().rearrange("(h p j) d -> h j p d", p=P, j=TT)
+    outr = out.flatten_outer_dims().rearrange("(h p j) d -> h p j d", p=P, j=TT)
     cosr = cos_t.rearrange("(p j) n -> j p n", j=TT)
     sinr = sin_t.rearrange("(p j) n -> j p n", j=TT)
     inv_sqrt_n = 1.0 / (float(N) ** 0.5)
 
     with ExitStack() as ctx:
         const = ctx.enter_context(tc.tile_pool(name="const", bufs=1))
+        tables = ctx.enter_context(tc.tile_pool(name="tables", bufs=2))
         xpool = ctx.enter_context(tc.tile_pool(name="xpool", bufs=AHEAD + 1))
         prod = ctx.enter_context(tc.tile_pool(name="prod", bufs=3))
         shared = ctx.enter_context(tc.tile_pool(name="shared", bufs=1))
-        qpool = ctx.enter_context(tc.tile_pool(name="qpool", bufs=2))
-        spool = ctx.enter_context(tc.tile_pool(name="spool", bufs=2))
+        spool = ctx.enter_context(tc.tile_pool(name="spool", bufs=3))
         tabp = ctx.enter_context(tc.psum_pool(name="tabp", bufs=1))
         accp = ctx.enter_context(tc.psum_pool(name="accp", bufs=3))
         scp = ctx.enter_context(tc.psum_pool(name="scp", bufs=1))
         op = ctx.enter_context(tc.psum_pool(name="op", bufs=1))
         ctx.enter_context(tc.manual_schedule())
 
+        ident_b = const.tile([P, P], BF16, name="ident_b")
+        make_identity(nc, ident_b[:])
         ident = const.tile([P, P], F32, name="ident")
         make_identity(nc, ident[:])
+        minus_b = const.tile([P, P], BF16, name="minus_b")
+        nc.scalar.mul(out=minus_b[:], in_=ident_b[:], mul=-1.0)
 
-        cos_sb = []
-        sin_sb = []
-        sneg = []
-        sodd = []
-        tab_t = []
-        for tau in range(TT):
-            cos_sb.append(const.tile([P, N], BF16, name="cos%d" % tau))
-            sin_sb.append(const.tile([P, N], BF16, name="sin%d" % tau))
-            sneg.append(const.tile([P, 2, NQ], BF16, name="sneg%d" % tau))
-            sodd.append(const.tile([P, 2, QV], BF16, name="sodd%d" % tau))
-            tab_t.append(const.tile([P, NTB, P], F32, name="tabt%d" % tau))
         kcodes = const.tile([P, H * TT, 512], U32, name="kcodes", align_bytes=64)
         kscales = const.tile([P, H * TT, 512], U8, name="kscales", align_bytes=64)
+        qcodes = const.tile([P, H * TT, 512], U32, name="qcodes", align_bytes=64)
+        qscales = const.tile([P, H * TT, 512], U8, name="qscales", align_bytes=64)
+        sg = const.tile([P, H * TT, P, 4], BF16, name="sg", align_bytes=64)
         v_raw = const.tile([P, 4, D], BF16, name="v_raw")
         v_grp = const.tile([P, D, 4], BF16, name="v_grp", align_bytes=64)
         vcodes = const.tile([P, D], U32, name="vcodes", align_bytes=64)
         vscales = const.tile([P, D], U8, name="vscales", align_bytes=64)
 
         units = []
-        for which in range(2):
-            for tau in range(TT):
+        for tau in range(TT):
+            for which in range(2):
                 for h in range(H):
                     units.append((which, tau, h))
         NU = len(units)
+        PER = 2 * H
         state = {}
 
-        def load_tables(tau):
-            nc.sync.dma_start(out=cos_sb[tau][:], in_=cosr[tau, :, :])
-            nc.sync.dma_start(out=sin_sb[tau][:], in_=sinr[tau, :, :])
+        def quad_view(ap):
+            return ap.rearrange("p (q j) -> p j q", j=4)
+
+        def load_cos(tau):
+            t = tables.tile([P, N], BF16, name="cos")
+            nc.sync.dma_start(out=t[:], in_=cosr[tau, :, :])
+            state[("cos", tau)] = t
+
+        def load_sin(tau):
+            t = tables.tile([P, N], BF16, name="sin")
+            nc.sync.dma_start(out=t[:], in_=sinr[tau, :, :])
+            state[("sin", tau)] = t
 
         def load(u):
             which, tau, h = units[u]
@@ -89,80 +96,59 @@ def tile_bidirectionalattention_pa_kernel(tc, Q, K, V, cos_t, sin_t, out):
             nc.sync.dma_start(out=x[:], in_=src[h, tau, :, :])
             state[("x", u)] = x
 
-        def quad_view(ap):
-            return ap.rearrange("p (q j) -> p j q", j=4)
-
         def arrange_sin(tau):
-            sv = quad_view(sin_sb[tau][:])
-            nc.scalar.mul(out=sneg[tau][:], in_=sv[:, 0:4:2, :], mul=-1.0)
-            nc.scalar.copy(out=sodd[tau][:], in_=sv[:, 1:4:2, 0:QV])
+            sv = quad_view(state[("sin", tau)][:])
+            g = tables.tile([P, 4, NQ - QV], BF16, name="gsin")
+            nc.scalar.copy(out=g[:, 0:4:2, :], in_=sv[:, 1:4:2, QV:NQ])
+            nc.scalar.mul(out=g[:, 1:4:2, :], in_=sv[:, 0:4:2, QV:NQ], mul=-1.0)
+            state[("gsin", tau)] = g
 
-        def tables_flip(tau):
-            cw = cos_sb[tau][:].bitcast(F32)
-            sw = sodd[tau][:].rearrange("p u q -> p (u q)").bitcast(F32)
-            for b0 in range(0, NTB, 4):
-                n = min(4, NTB - b0)
-                ps = accp.tile([P, 4, P], F32, name="ps")
-                for k in range(n):
-                    b = b0 + k
-                    srcw = cw[:, b * P : (b + 1) * P] if b < 8 else sw[:, (b - 8) * P : (b - 7) * P]
-                    nc.tensor.transpose(ps[:, k, :], srcw, ident[:])
-                nc.scalar.copy(out=tab_t[tau][:, b0 : b0 + n, :], in_=ps[:, 0:n, :])
+        def place_sin(tau):
+            t = tabp.tile([P, 2, 2 * QV], BF16, name="tabs")
+            sv = state[("sin", tau)][:].rearrange("p (i e) -> p e i", e=2)
+            nc.tensor.matmul(out=t[:, 0, :], lhsT=ident_b[:], rhs=sv[:, 1, 0 : 2 * QV], start=True, stop=True)
+            nc.tensor.matmul(out=t[:, 1, :], lhsT=minus_b[:], rhs=sv[:, 0, 0 : 2 * QV], start=True, stop=True)
+            state["tabs"] = t
 
-        def tables_back(tau, part):
-            if part == 0:
-                t = tabp.tile([P, 512], F32, name="tabc0")
-                blocks = range(0, 4)
-            elif part == 1:
-                t = tabp.tile([P, 512], F32, name="tabc1")
-                blocks = range(4, 8)
-            else:
-                t = tabp.tile([P, 512], F32, name="tabs")
-                blocks = range(8, NTB)
-            for k, b in enumerate(blocks):
-                nc.tensor.transpose(t[:, k * P : (k + 1) * P], tab_t[tau][:, b, :], ident[:])
-            state[("tab", part)] = t
+        def place_cos(tau, part):
+            t = tabp.tile([P, 2, 512], BF16, name="tabc%d" % part)
+            cv = state[("cos", tau)]
+            for k in range(2):
+                c0 = part * 1024 + k * 512
+                nc.tensor.matmul(out=t[:, k, :], lhsT=ident_b[:], rhs=cv[:, c0 : c0 + 512], start=True, stop=True)
+            state[("tabc", part)] = t
 
         def products_begin(u):
+            k = u % SLOTS
             a = prod.tile([P, 4, NQ], F32, name="a")
-            k = u % 3
             b = shared.tile([P, 4, NQ], F32, name="b%d" % k, offset=k * 16 * NQ, align_bytes=64)
             state[("ab", u)] = (a, b)
 
         def product_cos(u, part):
-            which, tau, h = units[u]
             xv = quad_view(state[("x", u)][:])
             a, b = state[("ab", u)]
             rng = slice(part * 256, (part + 1) * 256)
-            if u == 0:
-                cv = quad_view(cos_sb[tau][:])[:, :, rng]
-            else:
-                cv = quad_view(state[("tab", part)][:].bitcast(BF16))
+            cv = quad_view(state[("tabc", part)][:].rearrange("p k n -> p (k n)"))
             nc.vector.tensor_tensor(out=a[:, :, rng], in0=xv[:, :, rng], in1=cv, op=MULT)
 
         def product_sin_vector(u):
-            which, tau, h = units[u]
-            xv = quad_view(state[("x", u)][:])
+            xv = state[("x", u)][:].rearrange("p (q u e) -> p u e q", u=2, e=2)
             a, b = state[("ab", u)]
-            if u == 0:
-                sv = sodd[tau][:]
-            else:
-                sv = state[("tab", 2)][:].bitcast(BF16)[:, 0 : 2 * QV].rearrange("p (u q) -> p u q", u=2)
-            nc.vector.tensor_tensor(out=b[:, 1:4:2, 0:QV], in0=xv[:, 0:4:2, 0:QV], in1=sv, op=MULT)
+            bv = b[:].rearrange("p (u e) q -> p u e q", u=2)
+            sv = state["tabs"][:].rearrange("p e (q u) -> p u e q", u=2)
+            nc.vector.tensor_tensor(out=bv[:, :, :, 0:QV], in0=xv[:, :, :, 0:QV], in1=sv, op=MULT)
 
         def product_sin_gpsimd(u):
             which, tau, h = units[u]
             xv = quad_view(state[("x", u)][:])
-            sv = quad_view(sin_sb[tau][:])
             a, b = state[("ab", u)]
-            nc.gpsimd.tensor_tensor(out=b[:, 0:4:2, :], in0=xv[:, 1:4:2, :], in1=sneg[tau][:], op=MULT)
             nc.gpsimd.tensor_tensor(
-                out=b[:, 1:4:2, QV:NQ], in0=xv[:, 0:4:2, QV:NQ], in1=sv[:, 1:4:2, QV:NQ], op=MULT
+                out=b[:, :, QV:NQ], in0=xv[:, :, QV:NQ], in1=state[("gsin", tau)][:], op=MULT
             )
 
         def rotate_sum(u):
             a, b = state[("ab", u)]
-            k = (u + 2) % 3
+            k = (u + QUANT) % SLOTS
             grp = shared.tile([P, NG, P, 4], BF16, name="g%d" % k, offset=k * 16 * NQ, align_bytes=64)
             for g in range(NG):
                 ps = accp.tile([P, 4, P], F32, name="ps")
@@ -173,7 +159,7 @@ def tile_bidirectionalattention_pa_kernel(tc, Q, K, V, cos_t, sin_t, out):
                         out=dst, lhsT=a[:, j, cols], rhs=ident[:], start=True, stop=False, is_transpose=True
                     )
                     nc.tensor.matmul(
-                        out=dst, lhsT=b[:, j, cols], rhs=ident[:], start=False, stop=True, is_transpose=True
+                        out=dst, lhsT=b[:, j ^ 1, cols], rhs=ident[:], start=False, stop=True, is_transpose=True
                     )
                 nc.scalar.copy(out=grp[:, g, :, :], in_=ps[:].rearrange("p j t -> p t j"))
             state[("grp", u)] = grp
@@ -181,122 +167,130 @@ def tile_bidirectionalattention_pa_kernel(tc, Q, K, V, cos_t, sin_t, out):
         def quantise(u):
             which, tau, h = units[u]
             grp = state[("grp", u)]
-            if which == 0:
-                codes = kcodes[:, h * TT + tau, :]
-                scales = kscales[:, h * TT + tau, :]
-            else:
-                qc = qpool.tile([P, 512], U32, name="qc", align_bytes=64)
-                qs = qpool.tile([P, 512], U8, name="qs", align_bytes=64)
-                codes = qc[:]
-                scales = qs[:]
-                state[("q", u)] = (qc, qs)
+            codes = (kcodes if which == 0 else qcodes)[:, h * TT + tau, :]
+            scales = (kscales if which == 0 else qscales)[:, h * TT + tau, :]
             nc.vector.quantize_mx(
                 out=codes.bitcast(FP8X4), scales=scales, in_=grp[:].rearrange("p g t j -> p (g t j)")
             )
 
         def scores(u):
             which, tau, h = units[u]
-            qc, qs = state[("q", u)]
+            pairs = [(tau, t) for t in range(tau)] if which == 0 else [(t, tau) for t in range(tau + 1)]
+            if not pairs:
+                return
             sc = scp.tile([P, TT, P], F32, name="sc")
-            for tk in range(TT):
+            for i, (tk, tq) in enumerate(pairs):
                 for g in range(NG):
                     cols = slice(g * P, (g + 1) * P)
                     nc.tensor.matmul_mx(
-                        out=sc[:, tk, :],
+                        out=sc[:, i, :],
                         lhsT=kcodes[:, h * TT + tk, cols].bitcast(FP8X4),
                         lhsT_scale=kscales[:, h * TT + tk, cols],
-                        rhs=qc[:, cols].bitcast(FP8X4),
-                        rhs_scale=qs[:, cols],
+                        rhs=qcodes[:, h * TT + tq, cols].bitcast(FP8X4),
+                        rhs_scale=qscales[:, h * TT + tq, cols],
                         start=(g == 0),
                         stop=(g == NG - 1),
                     )
             state[("sc", u)] = sc
 
         def scores_out(u):
+            which, tau, h = units[u]
+            if ("sc", u) not in state:
+                return
             sc = state[("sc", u)]
-            sg = spool.tile([P, P, 4], BF16, name="sg", align_bytes=64)
-            nc.scalar.activation(out=sg[:], in_=sc[:].rearrange("p j q -> p q j"), func=COPY, scale=inv_sqrt_n)
-            state[("sg", u)] = sg
+            if which == 0:
+                dst = sg[:, h * TT : h * TT + tau, :, tau]
+                src = sc[:, 0:tau, :]
+            else:
+                dst = sg[:, h * TT + tau, :, 0 : tau + 1]
+                src = sc[:, 0 : tau + 1, :].rearrange("p j q -> p q j")
+            nc.scalar.activation(out=dst, in_=src, func=COPY, scale=inv_sqrt_n)
+
+        def finishes(u):
+            return 0 <= u < NU and units[u][1] == TT - 1
 
         def scores_quantise(u):
-            sg = state[("sg", u)]
-            scd = spool.tile([P, P], U32, name="scd", align_bytes=64)
-            ssc = spool.tile([P, P], U8, name="ssc", align_bytes=64)
-            nc.vector.quantize_mx(out=scd[:].bitcast(FP8X4), scales=ssc[:], in_=sg[:].rearrange("p q j -> p (q j)"))
+            which, tau, h = units[u]
+            i = h * TT + 2 * which
+            scd = spool.tile([P, 2 * P], U32, name="scd", align_bytes=64)
+            ssc = spool.tile([P, 2 * P], U8, name="ssc", align_bytes=64)
+            nc.vector.quantize_mx(
+                out=scd[:].bitcast(FP8X4), scales=ssc[:], in_=sg[:, i : i + 2, :, :].rearrange("p i q j -> p (i q j)")
+            )
             state[("scd", u)] = (scd, ssc)
 
         def values(u):
             scd, ssc = state[("scd", u)]
-            o_ps = op.tile([P, D], F32, name="o_ps")
-            nc.tensor.matmul_mx(
-                out=o_ps[:],
-                lhsT=scd[:].bitcast(FP8X4),
-                lhsT_scale=ssc[:],
-                rhs=vcodes[:].bitcast(FP8X4),
-                rhs_scale=vscales[:],
-                start=True,
-                stop=True,
-            )
+            o_ps = op.tile([P, 2, D], F32, name="o_ps")
+            for i in range(2):
+                cols = slice(i * P, (i + 1) * P)
+                nc.tensor.matmul_mx(
+                    out=o_ps[:, i, :],
+                    lhsT=scd[:, cols].bitcast(FP8X4),
+                    lhsT_scale=ssc[:, cols],
+                    rhs=vcodes[:].bitcast(FP8X4),
+                    rhs_scale=vscales[:],
+                    start=True,
+                    stop=True,
+                )
             state[("o", u)] = o_ps
 
         def store(u):
             which, tau, h = units[u]
             o_ps = state[("o", u)]
-            o_sb = spool.tile([P, D], F32, name="o_sb")
+            o_sb = spool.tile([P, 2, D], F32, name="o_sb")
             nc.scalar.copy(out=o_sb[:], in_=o_ps[:])
-            nc.sync.dma_start(out=outr[h, tau, :, :], in_=o_sb[:])
+            nc.sync.dma_start(out=outr[h, :, 2 * which : 2 * which + 2, :], in_=o_sb[:])
 
-        def is_q(u):
-            return 0 <= u < NU and units[u][0] == 1
-
-        nc.sync.dma_start(out=cos_sb[0][:], in_=cosr[0, :, :])
+        load_cos(0)
         load(0)
-        nc.sync.dma_start(out=sin_sb[0][:], in_=sinr[0, :, :])
+        load_sin(0)
         for u in range(1, AHEAD):
             load(u)
         nc.scalar.dma_start(out=v_raw[:], in_=Vf.rearrange("(p j) d -> p j d", j=TT))
-        nc.scalar.copy(out=v_grp[:], in_=v_raw[:].rearrange("p j d -> p d j"))
-        nc.vector.quantize_mx(
-            out=vcodes[:].bitcast(FP8X4), scales=vscales[:], in_=v_grp[:].rearrange("p d j -> p (d j)")
-        )
+        place_cos(0, 0)
+        place_cos(0, 1)
+        place_sin(0)
         arrange_sin(0)
-        tables_flip(0)
-        for part in range(3):
-            tables_back(0, part)
 
-        for s in range(NU + 5):
-            if s < NU and units[s][0] == 0 and units[s][2] == 0 and units[s][1] + 1 < TT:
-                load_tables(units[s][1] + 1)
+        for s in range(NU + FINISH):
+            tau = s // PER
+            if s % PER == 1 and tau + 1 < TT:
+                load_cos(tau + 1)
+                load_sin(tau + 1)
             if s + AHEAD < NU:
                 load(s + AHEAD)
-            last_of_phase = s < NU - 1 and units[s][2] == H - 1
-            next_tau = units[s + 1][1] if s < NU - 1 else 0
-            if 0 <= s - 2 < NU:
-                quantise(s - 2)
-            if is_q(s - 4):
-                scores_quantise(s - 4)
+            last_of_tau = s % PER == PER - 1 and tau + 1 < TT
+            if 0 <= s - QUANT < NU:
+                quantise(s - QUANT)
+            if finishes(s - FINISH):
+                scores_quantise(s - FINISH)
+            if s == PER:
+                nc.vector.quantize_mx(
+                    out=vcodes[:].bitcast(FP8X4), scales=vscales[:], in_=v_grp[:].rearrange("p d j -> p (d j)")
+                )
             if s < NU:
                 products_begin(s)
                 product_sin_gpsimd(s)
-                product_cos(s, 0)
-            if s < NU:
-                product_cos(s, 1)
                 product_sin_vector(s)
-            if s < NU and units[s][0] == 0 and units[s][2] == 2 and units[s][1] + 1 < TT:
-                arrange_sin(units[s][1] + 1)
-                tables_flip(units[s][1] + 1)
+                product_cos(s, 0)
+                product_cos(s, 1)
             if 0 <= s - 1 < NU:
                 rotate_sum(s - 1)
-            if last_of_phase:
-                tables_back(next_tau, 0)
-                tables_back(next_tau, 1)
-            if is_q(s - 2):
-                scores(s - 2)
-            if is_q(s - 4):
-                values(s - 4)
-            if last_of_phase:
-                tables_back(next_tau, 2)
-            if is_q(s - 2):
-                scores_out(s - 2)
-            if is_q(s - 4):
-                store(s - 4)
+            if last_of_tau:
+                place_sin(tau + 1)
+                place_cos(tau + 1, 0)
+            if 0 <= s - QUANT < NU:
+                scores(s - QUANT)
+            if finishes(s - FINISH):
+                values(s - FINISH)
+            if last_of_tau:
+                place_cos(tau + 1, 1)
+            if 0 <= s - QUANT < NU:
+                scores_out(s - QUANT)
+            if finishes(s - FINISH):
+                store(s - FINISH)
+            if s % PER == 4 and tau + 1 < TT:
+                arrange_sin(tau + 1)
+            if s == PER - 2:
+                nc.scalar.copy(out=v_grp[:], in_=v_raw[:].rearrange("p j d -> p d j"))

@@ -19,7 +19,7 @@ D = 256
 TT = T // P
 NG = N // 512
 NQ = N // 4
-QV = 208
+QV = NQ // 2
 AHEAD = 3
 SLOTS = 4
 QUANT = 3
@@ -88,6 +88,24 @@ def tile_bidirectionalattention_pa_kernel(tc, Q, K, V, cos_t, sin_t, out):
             t = tables.tile([P, N], BF16, name="sin")
             nc.sync.dma_start(out=t[:], in_=sinr[tau, :, :])
             state[("sin", tau)] = t
+
+        def load_first():
+            c = tables.tile([P, N], BF16, name="cos")
+            w = tables.tile([P, N], BF16, name="sin")
+            x = xpool.tile([P, N], BF16, name="x")
+            first, second = slice(0, N // 2), slice(N // 2, N)
+            for dst, src, cols in (
+                (x, Kr[0, 0, :, :], first),
+                (c, cosr[0, :, :], first),
+                (w, sinr[0, :, :], second),
+                (x, Kr[0, 0, :, :], second),
+                (c, cosr[0, :, :], second),
+                (w, sinr[0, :, :], first),
+            ):
+                nc.sync.dma_start(out=dst[:, cols], in_=src[:, cols])
+            state[("cos", 0)] = c
+            state[("sin", 0)] = w
+            state[("x", 0)] = x
 
         def load(u):
             which, tau, h = units[u]
@@ -242,12 +260,9 @@ def tile_bidirectionalattention_pa_kernel(tc, Q, K, V, cos_t, sin_t, out):
             nc.scalar.copy(out=o_sb[:], in_=o_ps[:])
             nc.sync.dma_start(out=outr[h, :, 2 * which : 2 * which + 2, :], in_=o_sb[:])
 
-        load_cos(0)
-        load(0)
-        load_sin(0)
+        load_first()
         for u in range(1, AHEAD):
             load(u)
-        nc.scalar.dma_start(out=v_raw[:], in_=Vf.rearrange("(p j) d -> p j d", j=TT))
         place_cos(0, 0)
         place_cos(0, 1)
         place_sin(0)
@@ -260,6 +275,8 @@ def tile_bidirectionalattention_pa_kernel(tc, Q, K, V, cos_t, sin_t, out):
                 load_sin(tau + 1)
             if s + AHEAD < NU:
                 load(s + AHEAD)
+            if s == 2:
+                nc.sync.dma_start(out=v_raw[:], in_=Vf.rearrange("(p j) d -> p j d", j=TT))
             last_of_tau = s % PER == PER - 1 and tau + 1 < TT
             if 0 <= s - QUANT < NU:
                 quantise(s - QUANT)
@@ -272,9 +289,12 @@ def tile_bidirectionalattention_pa_kernel(tc, Q, K, V, cos_t, sin_t, out):
             if s < NU:
                 products_begin(s)
                 product_sin_gpsimd(s)
-                product_sin_vector(s)
+                if s > 0:
+                    product_sin_vector(s)
                 product_cos(s, 0)
                 product_cos(s, 1)
+                if s == 0:
+                    product_sin_vector(s)
             if 0 <= s - 1 < NU:
                 rotate_sum(s - 1)
             if last_of_tau:

@@ -18,8 +18,8 @@ N = 2048
 D = 256
 TT = T // P
 NG = N // 512
-NQ = N // 4
-QV = NQ // 2
+NB = N // 32
+CV = 26
 AHEAD = 3
 SLOTS = 4
 QUANT = 3
@@ -76,8 +76,11 @@ def tile_bidirectionalattention_pa_kernel(tc, Q, K, V, cos_t, sin_t, out):
         PER = 2 * H
         state = {}
 
-        def quad_view(ap):
-            return ap.rearrange("p (q j) -> p j q", j=4)
+        def natural(ap):
+            return ap.rearrange("p (c j i e) -> p c j i e", j=4, i=4, e=2)
+
+        def by_slot(ap):
+            return ap.rearrange("p j (c i e) -> p c j i e", i=4, e=2)
 
         def load_cos(tau):
             t = tables.tile([P, N], BF16, name="cos")
@@ -93,16 +96,10 @@ def tile_bidirectionalattention_pa_kernel(tc, Q, K, V, cos_t, sin_t, out):
             c = tables.tile([P, N], BF16, name="cos")
             w = tables.tile([P, N], BF16, name="sin")
             x = xpool.tile([P, N], BF16, name="x")
-            first, second = slice(0, N // 2), slice(N // 2, N)
-            for dst, src, cols in (
-                (x, Kr[0, 0, :, :], first),
-                (c, cosr[0, :, :], first),
-                (w, sinr[0, :, :], second),
-                (x, Kr[0, 0, :, :], second),
-                (c, cosr[0, :, :], second),
-                (w, sinr[0, :, :], first),
-            ):
-                nc.sync.dma_start(out=dst[:, cols], in_=src[:, cols])
+            for cols in (slice(0, N // 2), slice(N // 2, N)):
+                nc.sync.dma_start(out=x[:, cols], in_=Kr[0, 0, :, cols])
+                nc.sync.dma_start(out=w[:, cols], in_=sinr[0, :, cols])
+                nc.sync.dma_start(out=c[:, cols], in_=cosr[0, :, cols])
             state[("cos", 0)] = c
             state[("sin", 0)] = w
             state[("x", 0)] = x
@@ -114,60 +111,66 @@ def tile_bidirectionalattention_pa_kernel(tc, Q, K, V, cos_t, sin_t, out):
             nc.sync.dma_start(out=x[:], in_=src[h, tau, :, :])
             state[("x", u)] = x
 
-        def arrange_sin(tau):
-            sv = quad_view(state[("sin", tau)][:])
-            g = tables.tile([P, 4, NQ - QV], BF16, name="gsin")
-            nc.scalar.copy(out=g[:, 0:4:2, :], in_=sv[:, 1:4:2, QV:NQ])
-            nc.scalar.mul(out=g[:, 1:4:2, :], in_=sv[:, 0:4:2, QV:NQ], mul=-1.0)
-            state[("gsin", tau)] = g
-
         def place_sin(tau):
-            t = tabp.tile([P, 2, 2 * QV], BF16, name="tabs")
-            sv = state[("sin", tau)][:].rearrange("p (i e) -> p e i", e=2)
-            nc.tensor.matmul(out=t[:, 0, :], lhsT=ident_b[:], rhs=sv[:, 1, 0 : 2 * QV], start=True, stop=True)
-            nc.tensor.matmul(out=t[:, 1, :], lhsT=minus_b[:], rhs=sv[:, 0, 0 : 2 * QV], start=True, stop=True)
+            t = tabp.tile([P, 32 * CV], BF16, name="tabs")
+            sv = state[("sin", tau)]
+            for c0 in range(0, 32 * CV, 512):
+                cols = slice(c0, min(c0 + 512, 32 * CV))
+                nc.tensor.matmul(out=t[:, cols], lhsT=ident_b[:], rhs=sv[:, cols], start=True, stop=True)
             state["tabs"] = t
 
         def place_cos(tau, part):
-            t = tabp.tile([P, 2, 512], BF16, name="tabc%d" % part)
+            t = tabp.tile([P, 2, N // 4], BF16, name="tabc%d" % part)
             cv = state[("cos", tau)]
-            for k in range(2):
-                c0 = part * 1024 + k * 512
-                nc.tensor.matmul(out=t[:, k, :], lhsT=ident_b[:], rhs=cv[:, c0 : c0 + 512], start=True, stop=True)
+            for e in range(2):
+                nc.tensor.matmul(
+                    out=t[:, e, :],
+                    lhsT=(minus_b if e == 0 else ident_b)[:],
+                    rhs=cv[:, part * N // 2 + e : (part + 1) * N // 2 : 2],
+                    start=True,
+                    stop=True,
+                )
             state[("tabc", part)] = t
 
         def products_begin(u):
             k = u % SLOTS
-            a = prod.tile([P, 4, NQ], F32, name="a")
-            b = shared.tile([P, 4, NQ], F32, name="b%d" % k, offset=k * 16 * NQ, align_bytes=64)
+            a = prod.tile([P, 4, 8 * NB], F32, name="a")
+            b = shared.tile([P, 4, 8 * NB], F32, name="b%d" % k, offset=k * 128 * NB, align_bytes=64)
             state[("ab", u)] = (a, b)
 
         def product_cos(u, part):
-            xv = quad_view(state[("x", u)][:])
             a, b = state[("ab", u)]
-            rng = slice(part * 256, (part + 1) * 256)
-            cv = quad_view(state[("tabc", part)][:].rearrange("p k n -> p (k n)"))
-            nc.vector.tensor_tensor(out=a[:, :, rng], in0=xv[:, :, rng], in1=cv, op=MULT)
+            cs = slice(part * NB // 2, (part + 1) * NB // 2)
+            nc.vector.tensor_tensor(
+                out=by_slot(a[:])[:, cs],
+                in0=natural(state[("x", u)][:])[:, cs],
+                in1=state[("tabc", part)][:].rearrange("p e (c j i) -> p c j i e", j=4, i=4),
+                op=MULT,
+            )
 
         def product_sin_vector(u):
-            xv = state[("x", u)][:].rearrange("p (q u e) -> p u e q", u=2, e=2)
             a, b = state[("ab", u)]
-            bv = b[:].rearrange("p (u e) q -> p u e q", u=2)
-            sv = state["tabs"][:].rearrange("p e (q u) -> p u e q", u=2)
-            nc.vector.tensor_tensor(out=bv[:, :, :, 0:QV], in0=xv[:, :, :, 0:QV], in1=sv, op=MULT)
+            nc.vector.tensor_tensor(
+                out=by_slot(b[:])[:, 0:CV],
+                in0=natural(state[("x", u)][:])[:, 0:CV, :, :, ::-1],
+                in1=natural(state["tabs"][:]),
+                op=MULT,
+            )
 
         def product_sin_gpsimd(u):
             which, tau, h = units[u]
-            xv = quad_view(state[("x", u)][:])
             a, b = state[("ab", u)]
             nc.gpsimd.tensor_tensor(
-                out=b[:, :, QV:NQ], in0=xv[:, :, QV:NQ], in1=state[("gsin", tau)][:], op=MULT
+                out=by_slot(b[:])[:, CV:NB],
+                in0=natural(state[("x", u)][:])[:, CV:NB, :, :, ::-1],
+                in1=natural(state[("sin", tau)][:])[:, CV:NB],
+                op=MULT,
             )
 
         def rotate_sum(u):
             a, b = state[("ab", u)]
             k = (u + QUANT) % SLOTS
-            grp = shared.tile([P, NG, P, 4], BF16, name="g%d" % k, offset=k * 16 * NQ, align_bytes=64)
+            grp = shared.tile([P, NG, P, 4], BF16, name="g%d" % k, offset=k * 128 * NB, align_bytes=64)
             for g in range(NG):
                 ps = accp.tile([P, 4, P], F32, name="ps")
                 cols = slice(g * P, (g + 1) * P)
@@ -177,7 +180,7 @@ def tile_bidirectionalattention_pa_kernel(tc, Q, K, V, cos_t, sin_t, out):
                         out=dst, lhsT=a[:, j, cols], rhs=ident[:], start=True, stop=False, is_transpose=True
                     )
                     nc.tensor.matmul(
-                        out=dst, lhsT=b[:, j ^ 1, cols], rhs=ident[:], start=False, stop=True, is_transpose=True
+                        out=dst, lhsT=b[:, j, cols], rhs=ident[:], start=False, stop=True, is_transpose=True
                     )
                 nc.scalar.copy(out=grp[:, g, :, :], in_=ps[:].rearrange("p j t -> p t j"))
             state[("grp", u)] = grp
@@ -263,10 +266,9 @@ def tile_bidirectionalattention_pa_kernel(tc, Q, K, V, cos_t, sin_t, out):
         load_first()
         for u in range(1, AHEAD):
             load(u)
+        place_sin(0)
         place_cos(0, 0)
         place_cos(0, 1)
-        place_sin(0)
-        arrange_sin(0)
 
         for s in range(NU + FINISH):
             tau = s // PER
@@ -289,12 +291,9 @@ def tile_bidirectionalattention_pa_kernel(tc, Q, K, V, cos_t, sin_t, out):
             if s < NU:
                 products_begin(s)
                 product_sin_gpsimd(s)
-                if s > 0:
-                    product_sin_vector(s)
+                product_sin_vector(s)
                 product_cos(s, 0)
                 product_cos(s, 1)
-                if s == 0:
-                    product_sin_vector(s)
             if 0 <= s - 1 < NU:
                 rotate_sum(s - 1)
             if last_of_tau:
@@ -310,7 +309,5 @@ def tile_bidirectionalattention_pa_kernel(tc, Q, K, V, cos_t, sin_t, out):
                 scores_out(s - QUANT)
             if finishes(s - FINISH):
                 store(s - FINISH)
-            if s % PER == 4 and tau + 1 < TT:
-                arrange_sin(tau + 1)
             if s == PER - 2:
                 nc.scalar.copy(out=v_grp[:], in_=v_raw[:].rearrange("p j d -> p d j"))

@@ -19,7 +19,7 @@ D = 256
 TT = T // P
 NG = N // 512
 NB = N // 32
-CV = 26
+CV = 32
 AHEAD = 3
 SLOTS = 4
 QUANT = 3
@@ -45,9 +45,7 @@ def tile_bidirectionalattention_pa_kernel(tc, Q, K, V, cos_t, sin_t, out):
         shared = ctx.enter_context(tc.tile_pool(name="shared", bufs=1))
         spool = ctx.enter_context(tc.tile_pool(name="spool", bufs=3))
         tabp = ctx.enter_context(tc.psum_pool(name="tabp", bufs=1))
-        accp = ctx.enter_context(tc.psum_pool(name="accp", bufs=3))
-        scp = ctx.enter_context(tc.psum_pool(name="scp", bufs=1))
-        op = ctx.enter_context(tc.psum_pool(name="op", bufs=1))
+        accp = ctx.enter_context(tc.psum_pool(name="accp", bufs=5))
         ctx.enter_context(tc.manual_schedule())
 
         ident_b = const.tile([P, P], BF16, name="ident_b")
@@ -199,7 +197,7 @@ def tile_bidirectionalattention_pa_kernel(tc, Q, K, V, cos_t, sin_t, out):
             pairs = [(tau, t) for t in range(tau)] if which == 0 else [(t, tau) for t in range(tau + 1)]
             if not pairs:
                 return
-            sc = scp.tile([P, TT, P], F32, name="sc")
+            sc = accp.tile([P, TT, P], F32, name="ps")
             for i, (tk, tq) in enumerate(pairs):
                 for g in range(NG):
                     cols = slice(g * P, (g + 1) * P)
@@ -242,7 +240,7 @@ def tile_bidirectionalattention_pa_kernel(tc, Q, K, V, cos_t, sin_t, out):
 
         def values(u):
             scd, ssc = state[("scd", u)]
-            o_ps = op.tile([P, 2, D], F32, name="o_ps")
+            o_ps = accp.tile([P, 2, D], F32, name="ps")
             for i in range(2):
                 cols = slice(i * P, (i + 1) * P)
                 nc.tensor.matmul_mx(

@@ -19,11 +19,10 @@ D = 256
 TT = T // P
 NG = N // 512
 NB = N // 32
-CV = 32
+CV = 24
 AHEAD = 3
-SLOTS = 4
-QUANT = 3
-FINISH = 5
+SLOTS = 5
+SINGLES = 4
 FLOPS = 2 * H * T * T * N + 2 * H * T * T * D
 
 
@@ -53,7 +52,7 @@ def tile_bidirectionalattention_pa_kernel(tc, Q, K, V, cos_t, sin_t, out):
         ident = const.tile([P, P], F32, name="ident")
         make_identity(nc, ident[:])
         minus_b = const.tile([P, P], BF16, name="minus_b")
-        nc.scalar.mul(out=minus_b[:], in_=ident_b[:], mul=-1.0)
+        nc.vector.tensor_scalar(out=minus_b[:], in0=ident_b[:], scalar1=-1.0, scalar2=None, op0=MULT)
 
         kcodes = const.tile([P, H * TT, 512], U32, name="kcodes", align_bytes=64)
         kscales = const.tile([P, H * TT, 512], U8, name="kscales", align_bytes=64)
@@ -72,6 +71,7 @@ def tile_bidirectionalattention_pa_kernel(tc, Q, K, V, cos_t, sin_t, out):
                     units.append((which, tau, h))
         NU = len(units)
         PER = 2 * H
+        PAIRED = NU - SINGLES
         state = {}
 
         def natural(ap):
@@ -93,42 +93,59 @@ def tile_bidirectionalattention_pa_kernel(tc, Q, K, V, cos_t, sin_t, out):
         def load_first():
             c = tables.tile([P, N], BF16, name="cos")
             w = tables.tile([P, N], BF16, name="sin")
-            x = xpool.tile([P, N], BF16, name="x")
-            for cols in (slice(0, N // 2), slice(N // 2, N)):
-                nc.sync.dma_start(out=x[:, cols], in_=Kr[0, 0, :, cols])
-                nc.sync.dma_start(out=w[:, cols], in_=sinr[0, :, cols])
+            pieces = []
+            for c0, c1 in ((0, 16), (16, 32), (32, NB)):
+                cols = slice(32 * c0, 32 * c1)
+                x = const.tile([P, 32 * (c1 - c0)], BF16, name="x%d" % c0)
                 nc.sync.dma_start(out=c[:, cols], in_=cosr[0, :, cols])
+                nc.sync.dma_start(out=x[:], in_=Kr[0, 0, :, cols])
+                nc.sync.dma_start(out=w[:, cols], in_=sinr[0, :, cols])
+                pieces.append((c0, c1, x))
             state[("cos", 0)] = c
             state[("sin", 0)] = w
-            state[("x", 0)] = x
+            state[("x", 0)] = pieces
 
         def load(u):
             which, tau, h = units[u]
             src = Kr if which == 0 else Qr
             x = xpool.tile([P, N], BF16, name="x")
             nc.sync.dma_start(out=x[:], in_=src[h, tau, :, :])
-            state[("x", u)] = x
+            state[("x", u)] = [(0, NB, x)]
 
-        def place_sin(tau):
-            t = tabp.tile([P, 32 * CV], BF16, name="tabs")
+        def x_blocks(u, c0, c1):
+            for p0, p1, x in state[("x", u)]:
+                if p0 <= c0 and c1 <= p1:
+                    return natural(x[:])[:, c0 - p0 : c1 - p0]
+            raise AssertionError
+
+        def place_begin(names):
+            for name in names:
+                if name == "tabs":
+                    state[name] = tabp.tile([P, 32 * CV], BF16, name="tabs")
+                elif name == "tabc0":
+                    state[name] = tabp.tile([P, 2, N // 4], BF16, name="tabc0")
+                else:
+                    state[name] = tabp.tile([P, 2, N // 4], BF16, name="tabc1")
+
+        def place_sin(tau, c0, c1):
+            t = state["tabs"]
             sv = state[("sin", tau)]
-            for c0 in range(0, 32 * CV, 512):
-                cols = slice(c0, min(c0 + 512, 32 * CV))
+            for k in range(c0, c1, 16):
+                cols = slice(32 * k, 32 * min(k + 16, c1))
                 nc.tensor.matmul(out=t[:, cols], lhsT=ident_b[:], rhs=sv[:, cols], start=True, stop=True)
-            state["tabs"] = t
 
-        def place_cos(tau, part):
-            t = tabp.tile([P, 2, N // 4], BF16, name="tabc%d" % part)
+        def place_cos(tau, c0, c1):
+            part = c0 // 32
+            t = state["tabc%d" % part]
             cv = state[("cos", tau)]
             for e in range(2):
                 nc.tensor.matmul(
-                    out=t[:, e, :],
+                    out=t[:, e, 16 * (c0 - 32 * part) : 16 * (c1 - 32 * part)],
                     lhsT=(minus_b if e == 0 else ident_b)[:],
-                    rhs=cv[:, part * N // 2 + e : (part + 1) * N // 2 : 2],
+                    rhs=cv[:, 32 * c0 + e : 32 * c1 : 2],
                     start=True,
                     stop=True,
                 )
-            state[("tabc", part)] = t
 
         def products_begin(u):
             k = u % SLOTS
@@ -136,39 +153,72 @@ def tile_bidirectionalattention_pa_kernel(tc, Q, K, V, cos_t, sin_t, out):
             b = shared.tile([P, 4, 8 * NB], F32, name="b%d" % k, offset=k * 128 * NB, align_bytes=64)
             state[("ab", u)] = (a, b)
 
-        def product_cos(u, part):
+        def product_cos(u, c0, c1):
             a, b = state[("ab", u)]
-            cs = slice(part * NB // 2, (part + 1) * NB // 2)
+            part = c0 // 32
+            cv = state["tabc%d" % part][:].rearrange("p e (c j i) -> p c j i e", j=4, i=4)
             nc.vector.tensor_tensor(
-                out=by_slot(a[:])[:, cs],
-                in0=natural(state[("x", u)][:])[:, cs],
-                in1=state[("tabc", part)][:].rearrange("p e (c j i) -> p c j i e", j=4, i=4),
+                out=by_slot(a[:])[:, c0:c1],
+                in0=x_blocks(u, c0, c1),
+                in1=cv[:, c0 - 32 * part : c1 - 32 * part],
                 op=MULT,
             )
 
-        def product_sin_vector(u):
+        def product_sin(engine, u, table, c0, c1):
             a, b = state[("ab", u)]
-            nc.vector.tensor_tensor(
-                out=by_slot(b[:])[:, 0:CV],
-                in0=natural(state[("x", u)][:])[:, 0:CV, :, :, ::-1],
-                in1=natural(state["tabs"][:]),
+            engine.tensor_tensor(
+                out=by_slot(b[:])[:, c0:c1],
+                in0=x_blocks(u, c0, c1)[:, :, :, :, ::-1],
+                in1=natural(table[:])[:, c0:c1],
                 op=MULT,
             )
 
-        def product_sin_gpsimd(u):
+        def products(u):
             which, tau, h = units[u]
-            a, b = state[("ab", u)]
-            nc.gpsimd.tensor_tensor(
-                out=by_slot(b[:])[:, CV:NB],
-                in0=natural(state[("x", u)][:])[:, CV:NB, :, :, ::-1],
-                in1=natural(state[("sin", tau)][:])[:, CV:NB],
-                op=MULT,
-            )
+            products_begin(u)
+            sin = state[("sin", tau)]
+            if u == 0:
+                product_sin(nc.gpsimd, u, sin, CV, 32)
+                product_sin(nc.gpsimd, u, sin, 32, NB)
+            elif u == NU - 1:
+                product_sin(nc.gpsimd, u, sin, CV, 48)
+                product_sin(nc.gpsimd, u, sin, 48, NB)
+            else:
+                product_sin(nc.gpsimd, u, sin, CV, NB)
+            tabs = state["tabs"]
+            if u == 0:
+                place_cos(0, 0, 16)
+                product_cos(u, 0, 16)
+                place_sin(0, 0, 16)
+                product_sin(nc.vector, u, tabs, 0, 16)
+                place_cos(0, 16, 32)
+                product_cos(u, 16, 32)
+                place_sin(0, 16, CV)
+                product_sin(nc.vector, u, tabs, 16, CV)
+                place_cos(0, 32, NB)
+                product_cos(u, 32, NB)
+            else:
+                product_sin(nc.vector, u, tabs, 0, CV)
+                product_cos(u, 0, 32)
+                if u == NU - 1:
+                    product_cos(u, 32, 48)
+                    product_cos(u, 48, NB)
+                else:
+                    product_cos(u, 32, NB)
 
         def rotate_sum(u):
             a, b = state[("ab", u)]
-            k = (u + QUANT) % SLOTS
-            grp = shared.tile([P, NG, P, 4], BF16, name="g%d" % k, offset=k * 128 * NB, align_bytes=64)
+            if u >= PAIRED:
+                k = (u + 3) % SLOTS
+                pair = shared.tile([P, 1, NG, P, 4], BF16, name="g%d" % k, offset=k * 128 * NB, align_bytes=64)
+                grp = pair[:, 0]
+            elif u % 2 == 0:
+                k = (u + 4) % SLOTS
+                pair = shared.tile([P, 2, NG, P, 4], BF16, name="g%d" % k, offset=k * 128 * NB, align_bytes=64)
+                grp = pair[:, 0]
+            else:
+                pair = state[("grp", u - 1)]
+                grp = pair[:, 1]
             for g in range(NG):
                 ps = accp.tile([P, 4, P], F32, name="ps")
                 cols = slice(g * P, (g + 1) * P)
@@ -181,16 +231,22 @@ def tile_bidirectionalattention_pa_kernel(tc, Q, K, V, cos_t, sin_t, out):
                         out=dst, lhsT=b[:, j, cols], rhs=ident[:], start=False, stop=True, is_transpose=True
                     )
                 nc.scalar.copy(out=grp[:, g, :, :], in_=ps[:].rearrange("p j t -> p t j"))
-            state[("grp", u)] = grp
+            state[("grp", u)] = pair
 
-        def quantise(u):
+        def quantise(u, n):
             which, tau, h = units[u]
-            grp = state[("grp", u)]
-            codes = (kcodes if which == 0 else qcodes)[:, h * TT + tau, :]
-            scales = (kscales if which == 0 else qscales)[:, h * TT + tau, :]
-            nc.vector.quantize_mx(
-                out=codes.bitcast(FP8X4), scales=scales, in_=grp[:].rearrange("p g t j -> p (g t j)")
-            )
+            i = tau * H + h
+            codes = (kcodes if which == 0 else qcodes)[:, i : i + n, :].rearrange("p u w -> p (u w)")
+            scales = (kscales if which == 0 else qscales)[:, i : i + n, :].rearrange("p u w -> p (u w)")
+            values_in = state[("grp", u)][:].rearrange("p u g t j -> p (u g t j)")
+            words = 512 * n
+            step = words // 2 if u == NU - 1 else words
+            for w in range(0, words, step):
+                nc.vector.quantize_mx(
+                    out=codes[:, w : w + step].bitcast(FP8X4),
+                    scales=scales[:, w : w + step],
+                    in_=values_in[:, 4 * w : 4 * (w + step)],
+                )
 
         def scores(u):
             which, tau, h = units[u]
@@ -203,14 +259,17 @@ def tile_bidirectionalattention_pa_kernel(tc, Q, K, V, cos_t, sin_t, out):
                     cols = slice(g * P, (g + 1) * P)
                     nc.tensor.matmul_mx(
                         out=sc[:, i, :],
-                        lhsT=kcodes[:, h * TT + tk, cols].bitcast(FP8X4),
-                        lhsT_scale=kscales[:, h * TT + tk, cols],
-                        rhs=qcodes[:, h * TT + tq, cols].bitcast(FP8X4),
-                        rhs_scale=qscales[:, h * TT + tq, cols],
+                        lhsT=kcodes[:, tk * H + h, cols].bitcast(FP8X4),
+                        lhsT_scale=kscales[:, tk * H + h, cols],
+                        rhs=qcodes[:, tq * H + h, cols].bitcast(FP8X4),
+                        rhs_scale=qscales[:, tq * H + h, cols],
                         start=(g == 0),
                         stop=(g == NG - 1),
                     )
             state[("sc", u)] = sc
+
+        def sg_index(h, tq):
+            return (tq // 2) * 2 * H + 2 * h + tq % 2
 
         def scores_out(u):
             which, tau, h = units[u]
@@ -218,33 +277,41 @@ def tile_bidirectionalattention_pa_kernel(tc, Q, K, V, cos_t, sin_t, out):
                 return
             sc = state[("sc", u)]
             if which == 0:
-                dst = sg[:, h * TT : h * TT + tau, :, tau]
-                src = sc[:, 0:tau, :]
+                for t0 in range(0, tau, 2):
+                    n = min(2, tau - t0)
+                    i = sg_index(h, t0)
+                    nc.scalar.activation(
+                        out=sg[:, i : i + n, :, tau], in_=sc[:, t0 : t0 + n, :], func=COPY, scale=inv_sqrt_n
+                    )
             else:
-                dst = sg[:, h * TT + tau, :, 0 : tau + 1]
-                src = sc[:, 0 : tau + 1, :].rearrange("p j q -> p q j")
-            nc.scalar.activation(out=dst, in_=src, func=COPY, scale=inv_sqrt_n)
+                nc.scalar.activation(
+                    out=sg[:, sg_index(h, tau), :, 0 : tau + 1],
+                    in_=sc[:, 0 : tau + 1, :].rearrange("p j q -> p q j"),
+                    func=COPY,
+                    scale=inv_sqrt_n,
+                )
 
-        def finishes(u):
-            return 0 <= u < NU and units[u][1] == TT - 1
-
-        def scores_quantise(u):
+        def scores_quantise(u, n):
             which, tau, h = units[u]
-            i = h * TT + 2 * which
-            scd = spool.tile([P, 2 * P], U32, name="scd", align_bytes=64)
-            ssc = spool.tile([P, 2 * P], U8, name="ssc", align_bytes=64)
+            i = sg_index(h, 2 * which)
+            scd = spool.tile([P, 2 * n * P], U32, name="scd", align_bytes=64)
+            ssc = spool.tile([P, 2 * n * P], U8, name="ssc", align_bytes=64)
             nc.vector.quantize_mx(
-                out=scd[:].bitcast(FP8X4), scales=ssc[:], in_=sg[:, i : i + 2, :, :].rearrange("p i q j -> p (i q j)")
+                out=scd[:].bitcast(FP8X4),
+                scales=ssc[:],
+                in_=sg[:, i : i + 2 * n, :, :].rearrange("p i q j -> p (i q j)"),
             )
-            state[("scd", u)] = (scd, ssc)
+            for k in range(n):
+                state[("scd", u + k)] = (scd, ssc, 2 * k * P)
 
         def values(u):
-            scd, ssc = state[("scd", u)]
-            o_ps = accp.tile([P, 2, D], F32, name="ps")
+            scd, ssc, w0 = state[("scd", u)]
+            last = u == NU - 1
+            tiles = [accp.tile([P, 2, D], F32, name="ps") for i in range(2 if last else 1)]
             for i in range(2):
-                cols = slice(i * P, (i + 1) * P)
+                cols = slice(w0 + i * P, w0 + (i + 1) * P)
                 nc.tensor.matmul_mx(
-                    out=o_ps[:, i, :],
+                    out=tiles[i if last else 0][:, i, :],
                     lhsT=scd[:, cols].bitcast(FP8X4),
                     lhsT_scale=ssc[:, cols],
                     rhs=vcodes[:].bitcast(FP8X4),
@@ -252,23 +319,35 @@ def tile_bidirectionalattention_pa_kernel(tc, Q, K, V, cos_t, sin_t, out):
                     start=True,
                     stop=True,
                 )
-            state[("o", u)] = o_ps
+            state[("o", u)] = tiles
 
         def store(u):
             which, tau, h = units[u]
-            o_ps = state[("o", u)]
+            tiles = state[("o", u)]
             o_sb = spool.tile([P, 2, D], F32, name="o_sb")
-            nc.scalar.copy(out=o_sb[:], in_=o_ps[:])
-            nc.sync.dma_start(out=outr[h, :, 2 * which : 2 * which + 2, :], in_=o_sb[:])
+            rows = outr[h, :, 2 * which : 2 * which + 2, :]
+            if u == NU - 1:
+                nc.scalar.copy(out=o_sb[:, 0, :], in_=tiles[0][:, 0, :])
+                nc.sync.dma_start(out=rows[:, 0, :], in_=o_sb[:, 0, :])
+                nc.vector.tensor_copy(out=o_sb[:, 1, :], in_=tiles[1][:, 1, :])
+                nc.scalar.dma_start(out=rows[:, 1, :], in_=o_sb[:, 1, :])
+            else:
+                nc.scalar.copy(out=o_sb[:], in_=tiles[0][:])
+                nc.sync.dma_start(out=rows, in_=o_sb[:])
 
         load_first()
         for u in range(1, AHEAD):
             load(u)
-        place_sin(0)
-        place_cos(0, 0)
-        place_cos(0, 1)
+        place_begin(("tabc0", "tabs", "tabc1"))
 
-        for s in range(NU + FINISH):
+        quantised = {}
+        finished = {}
+        for u in range(NU):
+            quantised.setdefault(u + 3 if u >= PAIRED else u // 2 * 2 + 4, []).append(u)
+            if units[u][1] == TT - 1:
+                finished.setdefault(u + 5 if u >= PAIRED else u // 2 * 2 + 6, []).append(u)
+
+        for s in range(NU + 5):
             tau = s // PER
             if s % PER == 1 and tau + 1 < TT:
                 load_cos(tau + 1)
@@ -278,34 +357,33 @@ def tile_bidirectionalattention_pa_kernel(tc, Q, K, V, cos_t, sin_t, out):
             if s == 2:
                 nc.sync.dma_start(out=v_raw[:], in_=Vf.rearrange("(p j) d -> p j d", j=TT))
             last_of_tau = s % PER == PER - 1 and tau + 1 < TT
-            if 0 <= s - QUANT < NU:
-                quantise(s - QUANT)
-            if finishes(s - FINISH):
-                scores_quantise(s - FINISH)
+            now = quantised.get(s, [])
+            end = finished.get(s, [])
+            if now:
+                quantise(now[0], len(now))
+            if end:
+                scores_quantise(end[0], len(end))
             if s == PER:
                 nc.vector.quantize_mx(
                     out=vcodes[:].bitcast(FP8X4), scales=vscales[:], in_=v_grp[:].rearrange("p d j -> p (d j)")
                 )
             if s < NU:
-                products_begin(s)
-                product_sin_gpsimd(s)
-                product_sin_vector(s)
-                product_cos(s, 0)
-                product_cos(s, 1)
+                products(s)
             if 0 <= s - 1 < NU:
                 rotate_sum(s - 1)
             if last_of_tau:
-                place_sin(tau + 1)
-                place_cos(tau + 1, 0)
-            if 0 <= s - QUANT < NU:
-                scores(s - QUANT)
-            if finishes(s - FINISH):
-                values(s - FINISH)
+                place_begin(("tabs", "tabc0", "tabc1"))
+                place_sin(tau + 1, 0, CV)
+                place_cos(tau + 1, 0, 32)
+            for u in now:
+                scores(u)
+            for u in end:
+                values(u)
             if last_of_tau:
-                place_cos(tau + 1, 1)
-            if 0 <= s - QUANT < NU:
-                scores_out(s - QUANT)
-            if finishes(s - FINISH):
-                store(s - FINISH)
+                place_cos(tau + 1, 32, NB)
+            for u in now:
+                scores_out(u)
+            for u in end:
+                store(u)
             if s == PER - 2:
                 nc.scalar.copy(out=v_grp[:], in_=v_raw[:].rearrange("p j d -> p d j"))

@@ -9,6 +9,7 @@ U32 = mybir.dt.uint32
 U8 = mybir.dt.uint8
 FP8X4 = mybir.dt.float8_e4m3fn_x4
 MULT = mybir.AluOpType.mult
+ADD = mybir.AluOpType.add
 COPY = mybir.ActivationFunctionType.Copy
 
 P = 128
@@ -19,7 +20,7 @@ D = 256
 TT = T // P
 NG = N // 512
 NB = N // 32
-CV = 24
+CV = 22
 AHEAD = 3
 SLOTS = 5
 SINGLES = 4
@@ -43,6 +44,7 @@ def tile_bidirectionalattention_pa_kernel(tc, Q, K, V, cos_t, sin_t, out):
         prod = ctx.enter_context(tc.tile_pool(name="prod", bufs=3))
         shared = ctx.enter_context(tc.tile_pool(name="shared", bufs=1))
         spool = ctx.enter_context(tc.tile_pool(name="spool", bufs=3))
+        outs = ctx.enter_context(tc.tile_pool(name="outs", bufs=6))
         tabp = ctx.enter_context(tc.psum_pool(name="tabp", bufs=1))
         accp = ctx.enter_context(tc.psum_pool(name="accp", bufs=5))
         ctx.enter_context(tc.manual_schedule())
@@ -206,6 +208,14 @@ def tile_bidirectionalattention_pa_kernel(tc, Q, K, V, cos_t, sin_t, out):
                 else:
                     product_cos(u, 32, NB)
 
+        def sum_on_vector(u):
+            a, b = state[("ab", u)]
+            for g in range(NG):
+                cols = slice(g * P, (g + 1) * P)
+                r = const.tile([P, 4, P], BF16, name="r%d" % g)
+                nc.vector.tensor_tensor(out=r[:], in0=a[:, :, cols], in1=b[:, :, cols], op=ADD)
+                state[("r", g)] = r
+
         def rotate_sum(u):
             a, b = state[("ab", u)]
             if u >= PAIRED:
@@ -220,6 +230,12 @@ def tile_bidirectionalattention_pa_kernel(tc, Q, K, V, cos_t, sin_t, out):
                 pair = state[("grp", u - 1)]
                 grp = pair[:, 1]
             for g in range(NG):
+                if u == NU - 1:
+                    ps = accp.tile([P, 4, P], BF16, name="ps")
+                    for j in range(4):
+                        nc.tensor.transpose(ps[:, j, :], state[("r", g)][:, j, :], ident_b[:])
+                    nc.scalar.copy(out=grp[:, g, :, :], in_=ps[:].rearrange("p j t -> p t j"))
+                    continue
                 ps = accp.tile([P, 4, P], F32, name="ps")
                 cols = slice(g * P, (g + 1) * P)
                 for j in range(4):
@@ -324,7 +340,7 @@ def tile_bidirectionalattention_pa_kernel(tc, Q, K, V, cos_t, sin_t, out):
         def store(u):
             which, tau, h = units[u]
             tiles = state[("o", u)]
-            o_sb = spool.tile([P, 2, D], F32, name="o_sb")
+            o_sb = outs.tile([P, 2, D], F32, name="o_sb")
             rows = outr[h, :, 2 * which : 2 * which + 2, :]
             if u == NU - 1:
                 nc.scalar.copy(out=o_sb[:, 0, :], in_=tiles[0][:, 0, :])
@@ -332,7 +348,10 @@ def tile_bidirectionalattention_pa_kernel(tc, Q, K, V, cos_t, sin_t, out):
                 nc.vector.tensor_copy(out=o_sb[:, 1, :], in_=tiles[1][:, 1, :])
                 nc.scalar.dma_start(out=rows[:, 1, :], in_=o_sb[:, 1, :])
             else:
-                nc.scalar.copy(out=o_sb[:], in_=tiles[0][:])
+                if u == NU - 2:
+                    nc.vector.tensor_copy(out=o_sb[:], in_=tiles[0][:])
+                else:
+                    nc.scalar.copy(out=o_sb[:], in_=tiles[0][:])
                 nc.sync.dma_start(out=rows, in_=o_sb[:])
 
         load_first()
@@ -343,11 +362,16 @@ def tile_bidirectionalattention_pa_kernel(tc, Q, K, V, cos_t, sin_t, out):
         quantised = {}
         finished = {}
         for u in range(NU):
-            quantised.setdefault(u + 3 if u >= PAIRED else u // 2 * 2 + 4, []).append(u)
+            if u < PAIRED:
+                quantised.setdefault(u // 2 * 2 + 4, []).append(u)
+            elif u > PAIRED:
+                quantised.setdefault(u + 2, []).append(u)
+            else:
+                quantised.setdefault(u + 3, []).append(u)
             if units[u][1] == TT - 1:
-                finished.setdefault(u + 5 if u >= PAIRED else u // 2 * 2 + 6, []).append(u)
+                finished.setdefault(u // 2 * 2 + (6 if u < PAIRED else 5) if u < NU - 2 else u + 4, []).append(u)
 
-        for s in range(NU + 5):
+        for s in range(NU + 4):
             tau = s // PER
             if s % PER == 1 and tau + 1 < TT:
                 load_cos(tau + 1)
@@ -360,7 +384,7 @@ def tile_bidirectionalattention_pa_kernel(tc, Q, K, V, cos_t, sin_t, out):
             now = quantised.get(s, [])
             end = finished.get(s, [])
             if now:
-                quantise(now[0], len(now))
+                quantise(now[0], 2 if now[0] < PAIRED else 1)
             if end:
                 scores_quantise(end[0], len(end))
             if s == PER:
@@ -369,6 +393,9 @@ def tile_bidirectionalattention_pa_kernel(tc, Q, K, V, cos_t, sin_t, out):
                 )
             if s < NU:
                 products(s)
+            if s == NU - 1:
+                quantise(now[1], 1)
+                sum_on_vector(s)
             if 0 <= s - 1 < NU:
                 rotate_sum(s - 1)
             if last_of_tau:
@@ -384,6 +411,9 @@ def tile_bidirectionalattention_pa_kernel(tc, Q, K, V, cos_t, sin_t, out):
             for u in now:
                 scores_out(u)
             for u in end:
-                store(u)
+                if u == NU - 1:
+                    store(u - 1)
+                if u != NU - 2:
+                    store(u)
             if s == PER - 2:
                 nc.scalar.copy(out=v_grp[:], in_=v_raw[:].rearrange("p j d -> p d j"))

@@ -20,7 +20,7 @@ D = 256
 TT = T // P
 NG = N // 512
 NB = N // 32
-CV = 22
+CV = 23
 AHEAD = 3
 SLOTS = 5
 SINGLES = 4

from contextlib import ExitStack

import concourse.mybir as mybir
from concourse.masks import make_identity

F32 = mybir.dt.float32
BF16 = mybir.dt.bfloat16
U32 = mybir.dt.uint32
U8 = mybir.dt.uint8
FP8X4 = mybir.dt.float8_e4m3fn_x4
MULT = mybir.AluOpType.mult
ADD = mybir.AluOpType.add
COPY = mybir.ActivationFunctionType.Copy

P = 128
H = 4
T = 512
N = 2048
D = 256
TT = T // P
NG = N // 512
NB = N // 32
CV = 23
AHEAD = 3
SLOTS = 5
SINGLES = 4
FLOPS = 2 * H * T * T * N + 2 * H * T * T * D


def tile_bidirectionalattention_pa_kernel(tc, Q, K, V, cos_t, sin_t, out):
    nc = tc.nc
    Qr = Q.flatten_outer_dims().rearrange("(h p j) n -> h j p n", p=P, j=TT)
    Kr = K.flatten_outer_dims().rearrange("(h p j) n -> h j p n", p=P, j=TT)
    Vf = V.flatten_outer_dims()
    outr = out.flatten_outer_dims().rearrange("(h p j) d -> h p j d", p=P, j=TT)
    cosr = cos_t.rearrange("(p j) n -> j p n", j=TT)
    sinr = sin_t.rearrange("(p j) n -> j p n", j=TT)
    inv_sqrt_n = 1.0 / (float(N) ** 0.5)

    with ExitStack() as ctx:
        const = ctx.enter_context(tc.tile_pool(name="const", bufs=1))
        tables = ctx.enter_context(tc.tile_pool(name="tables", bufs=2))
        xpool = ctx.enter_context(tc.tile_pool(name="xpool", bufs=AHEAD + 1))
        prod = ctx.enter_context(tc.tile_pool(name="prod", bufs=3))
        shared = ctx.enter_context(tc.tile_pool(name="shared", bufs=1))
        spool = ctx.enter_context(tc.tile_pool(name="spool", bufs=3))
        outs = ctx.enter_context(tc.tile_pool(name="outs", bufs=6))
        tabp = ctx.enter_context(tc.psum_pool(name="tabp", bufs=1))
        accp = ctx.enter_context(tc.psum_pool(name="accp", bufs=5))
        ctx.enter_context(tc.manual_schedule())

        ident_b = const.tile([P, P], BF16, name="ident_b")
        make_identity(nc, ident_b[:])
        ident = const.tile([P, P], F32, name="ident")
        make_identity(nc, ident[:])
        minus_b = const.tile([P, P], BF16, name="minus_b")
        nc.vector.tensor_scalar(out=minus_b[:], in0=ident_b[:], scalar1=-1.0, scalar2=None, op0=MULT)

        kcodes = const.tile([P, H * TT, 512], U32, name="kcodes", align_bytes=64)
        kscales = const.tile([P, H * TT, 512], U8, name="kscales", align_bytes=64)
        qcodes = const.tile([P, H * TT, 512], U32, name="qcodes", align_bytes=64)
        qscales = const.tile([P, H * TT, 512], U8, name="qscales", align_bytes=64)
        sg = const.tile([P, H * TT, P, 4], BF16, name="sg", align_bytes=64)
        v_raw = const.tile([P, 4, D], BF16, name="v_raw")
        v_grp = const.tile([P, D, 4], BF16, name="v_grp", align_bytes=64)
        vcodes = const.tile([P, D], U32, name="vcodes", align_bytes=64)
        vscales = const.tile([P, D], U8, name="vscales", align_bytes=64)

        units = []
        for tau in range(TT):
            for which in range(2):
                for h in range(H):
                    units.append((which, tau, h))
        NU = len(units)
        PER = 2 * H
        PAIRED = NU - SINGLES
        state = {}

        def natural(ap):
            return ap.rearrange("p (c j i e) -> p c j i e", j=4, i=4, e=2)

        def by_slot(ap):
            return ap.rearrange("p j (c i e) -> p c j i e", i=4, e=2)

        def load_cos(tau):
            t = tables.tile([P, N], BF16, name="cos")
            nc.sync.dma_start(out=t[:], in_=cosr[tau, :, :])
            state[("cos", tau)] = t

        def load_sin(tau):
            t = tables.tile([P, N], BF16, name="sin")
            nc.sync.dma_start(out=t[:], in_=sinr[tau, :, :])
            state[("sin", tau)] = t

        def load_first():
            c = tables.tile([P, N], BF16, name="cos")
            w = tables.tile([P, N], BF16, name="sin")
            pieces = []
            for c0, c1 in ((0, 16), (16, 32), (32, NB)):
                cols = slice(32 * c0, 32 * c1)
                x = const.tile([P, 32 * (c1 - c0)], BF16, name="x%d" % c0)
                nc.sync.dma_start(out=c[:, cols], in_=cosr[0, :, cols])
                nc.sync.dma_start(out=x[:], in_=Kr[0, 0, :, cols])
                nc.sync.dma_start(out=w[:, cols], in_=sinr[0, :, cols])
                pieces.append((c0, c1, x))
            state[("cos", 0)] = c
            state[("sin", 0)] = w
            state[("x", 0)] = pieces

        def load(u):
            which, tau, h = units[u]
            src = Kr if which == 0 else Qr
            x = xpool.tile([P, N], BF16, name="x")
            nc.sync.dma_start(out=x[:], in_=src[h, tau, :, :])
            state[("x", u)] = [(0, NB, x)]

        def x_blocks(u, c0, c1):
            for p0, p1, x in state[("x", u)]:
                if p0 <= c0 and c1 <= p1:
                    return natural(x[:])[:, c0 - p0 : c1 - p0]
            raise AssertionError

        def place_begin(names):
            for name in names:
                if name == "tabs":
                    state[name] = tabp.tile([P, 32 * CV], BF16, name="tabs")
                elif name == "tabc0":
                    state[name] = tabp.tile([P, 2, N // 4], BF16, name="tabc0")
                else:
                    state[name] = tabp.tile([P, 2, N // 4], BF16, name="tabc1")

        def place_sin(tau, c0, c1):
            t = state["tabs"]
            sv = state[("sin", tau)]
            for k in range(c0, c1, 16):
                cols = slice(32 * k, 32 * min(k + 16, c1))
                nc.tensor.matmul(out=t[:, cols], lhsT=ident_b[:], rhs=sv[:, cols], start=True, stop=True)

        def place_cos(tau, c0, c1):
            part = c0 // 32
            t = state["tabc%d" % part]
            cv = state[("cos", tau)]
            for e in range(2):
                nc.tensor.matmul(
                    out=t[:, e, 16 * (c0 - 32 * part) : 16 * (c1 - 32 * part)],
                    lhsT=(minus_b if e == 0 else ident_b)[:],
                    rhs=cv[:, 32 * c0 + e : 32 * c1 : 2],
                    start=True,
                    stop=True,
                )

        def products_begin(u):
            k = u % SLOTS
            a = prod.tile([P, 4, 8 * NB], F32, name="a")
            b = shared.tile([P, 4, 8 * NB], F32, name="b%d" % k, offset=k * 128 * NB, align_bytes=64)
            state[("ab", u)] = (a, b)

        def product_cos(u, c0, c1):
            a, b = state[("ab", u)]
            part = c0 // 32
            cv = state["tabc%d" % part][:].rearrange("p e (c j i) -> p c j i e", j=4, i=4)
            nc.vector.tensor_tensor(
                out=by_slot(a[:])[:, c0:c1],
                in0=x_blocks(u, c0, c1),
                in1=cv[:, c0 - 32 * part : c1 - 32 * part],
                op=MULT,
            )

        def product_sin(engine, u, table, c0, c1):
            a, b = state[("ab", u)]
            engine.tensor_tensor(
                out=by_slot(b[:])[:, c0:c1],
                in0=x_blocks(u, c0, c1)[:, :, :, :, ::-1],
                in1=natural(table[:])[:, c0:c1],
                op=MULT,
            )

        def products(u):
            which, tau, h = units[u]
            products_begin(u)
            sin = state[("sin", tau)]
            if u == 0:
                product_sin(nc.gpsimd, u, sin, CV, 32)
                product_sin(nc.gpsimd, u, sin, 32, NB)
            elif u == NU - 1:
                product_sin(nc.gpsimd, u, sin, CV, 48)
                product_sin(nc.gpsimd, u, sin, 48, NB)
            else:
                product_sin(nc.gpsimd, u, sin, CV, NB)
            tabs = state["tabs"]
            if u == 0:
                place_cos(0, 0, 16)
                product_cos(u, 0, 16)
                place_sin(0, 0, 16)
                product_sin(nc.vector, u, tabs, 0, 16)
                place_cos(0, 16, 32)
                product_cos(u, 16, 32)
                place_sin(0, 16, CV)
                product_sin(nc.vector, u, tabs, 16, CV)
                place_cos(0, 32, NB)
                product_cos(u, 32, NB)
            else:
                product_sin(nc.vector, u, tabs, 0, CV)
                product_cos(u, 0, 32)
                if u == NU - 1:
                    product_cos(u, 32, 48)
                    product_cos(u, 48, NB)
                else:
                    product_cos(u, 32, NB)

        def sum_on_vector(u):
            a, b = state[("ab", u)]
            for g in range(NG):
                cols = slice(g * P, (g + 1) * P)
                r = const.tile([P, 4, P], BF16, name="r%d" % g)
                nc.vector.tensor_tensor(out=r[:], in0=a[:, :, cols], in1=b[:, :, cols], op=ADD)
                state[("r", g)] = r

        def rotate_sum(u):
            a, b = state[("ab", u)]
            if u >= PAIRED:
                k = (u + 3) % SLOTS
                pair = shared.tile([P, 1, NG, P, 4], BF16, name="g%d" % k, offset=k * 128 * NB, align_bytes=64)
                grp = pair[:, 0]
            elif u % 2 == 0:
                k = (u + 4) % SLOTS
                pair = shared.tile([P, 2, NG, P, 4], BF16, name="g%d" % k, offset=k * 128 * NB, align_bytes=64)
                grp = pair[:, 0]
            else:
                pair = state[("grp", u - 1)]
                grp = pair[:, 1]
            for g in range(NG):
                if u == NU - 1:
                    ps = accp.tile([P, 4, P], BF16, name="ps")
                    for j in range(4):
                        nc.tensor.transpose(ps[:, j, :], state[("r", g)][:, j, :], ident_b[:])
                    nc.scalar.copy(out=grp[:, g, :, :], in_=ps[:].rearrange("p j t -> p t j"))
                    continue
                ps = accp.tile([P, 4, P], F32, name="ps")
                cols = slice(g * P, (g + 1) * P)
                for j in range(4):
                    dst = ps[:, j, :]
                    nc.tensor.matmul(
                        out=dst, lhsT=a[:, j, cols], rhs=ident[:], start=True, stop=False, is_transpose=True
                    )
                    nc.tensor.matmul(
                        out=dst, lhsT=b[:, j, cols], rhs=ident[:], start=False, stop=True, is_transpose=True
                    )
                nc.scalar.copy(out=grp[:, g, :, :], in_=ps[:].rearrange("p j t -> p t j"))
            state[("grp", u)] = pair

        def quantise(u, n):
            which, tau, h = units[u]
            i = tau * H + h
            codes = (kcodes if which == 0 else qcodes)[:, i : i + n, :].rearrange("p u w -> p (u w)")
            scales = (kscales if which == 0 else qscales)[:, i : i + n, :].rearrange("p u w -> p (u w)")
            values_in = state[("grp", u)][:].rearrange("p u g t j -> p (u g t j)")
            words = 512 * n
            step = words // 2 if u == NU - 1 else words
            for w in range(0, words, step):
                nc.vector.quantize_mx(
                    out=codes[:, w : w + step].bitcast(FP8X4),
                    scales=scales[:, w : w + step],
                    in_=values_in[:, 4 * w : 4 * (w + step)],
                )

        def scores(u):
            which, tau, h = units[u]
            pairs = [(tau, t) for t in range(tau)] if which == 0 else [(t, tau) for t in range(tau + 1)]
            if not pairs:
                return
            sc = accp.tile([P, TT, P], F32, name="ps")
            for i, (tk, tq) in enumerate(pairs):
                for g in range(NG):
                    cols = slice(g * P, (g + 1) * P)
                    nc.tensor.matmul_mx(
                        out=sc[:, i, :],
                        lhsT=kcodes[:, tk * H + h, cols].bitcast(FP8X4),
                        lhsT_scale=kscales[:, tk * H + h, cols],
                        rhs=qcodes[:, tq * H + h, cols].bitcast(FP8X4),
                        rhs_scale=qscales[:, tq * H + h, cols],
                        start=(g == 0),
                        stop=(g == NG - 1),
                    )
            state[("sc", u)] = sc

        def sg_index(h, tq):
            return (tq // 2) * 2 * H + 2 * h + tq % 2

        def scores_out(u):
            which, tau, h = units[u]
            if ("sc", u) not in state:
                return
            sc = state[("sc", u)]
            if which == 0:
                for t0 in range(0, tau, 2):
                    n = min(2, tau - t0)
                    i = sg_index(h, t0)
                    nc.scalar.activation(
                        out=sg[:, i : i + n, :, tau], in_=sc[:, t0 : t0 + n, :], func=COPY, scale=inv_sqrt_n
                    )
            else:
                nc.scalar.activation(
                    out=sg[:, sg_index(h, tau), :, 0 : tau + 1],
                    in_=sc[:, 0 : tau + 1, :].rearrange("p j q -> p q j"),
                    func=COPY,
                    scale=inv_sqrt_n,
                )

        def scores_quantise(u, n):
            which, tau, h = units[u]
            i = sg_index(h, 2 * which)
            scd = spool.tile([P, 2 * n * P], U32, name="scd", align_bytes=64)
            ssc = spool.tile([P, 2 * n * P], U8, name="ssc", align_bytes=64)
            nc.vector.quantize_mx(
                out=scd[:].bitcast(FP8X4),
                scales=ssc[:],
                in_=sg[:, i : i + 2 * n, :, :].rearrange("p i q j -> p (i q j)"),
            )
            for k in range(n):
                state[("scd", u + k)] = (scd, ssc, 2 * k * P)

        def values(u):
            scd, ssc, w0 = state[("scd", u)]
            last = u == NU - 1
            tiles = [accp.tile([P, 2, D], F32, name="ps") for i in range(2 if last else 1)]
            for i in range(2):
                cols = slice(w0 + i * P, w0 + (i + 1) * P)
                nc.tensor.matmul_mx(
                    out=tiles[i if last else 0][:, i, :],
                    lhsT=scd[:, cols].bitcast(FP8X4),
                    lhsT_scale=ssc[:, cols],
                    rhs=vcodes[:].bitcast(FP8X4),
                    rhs_scale=vscales[:],
                    start=True,
                    stop=True,
                )
            state[("o", u)] = tiles

        def store(u):
            which, tau, h = units[u]
            tiles = state[("o", u)]
            o_sb = outs.tile([P, 2, D], F32, name="o_sb")
            rows = outr[h, :, 2 * which : 2 * which + 2, :]
            if u == NU - 1:
                nc.scalar.copy(out=o_sb[:, 0, :], in_=tiles[0][:, 0, :])
                nc.sync.dma_start(out=rows[:, 0, :], in_=o_sb[:, 0, :])
                nc.vector.tensor_copy(out=o_sb[:, 1, :], in_=tiles[1][:, 1, :])
                nc.scalar.dma_start(out=rows[:, 1, :], in_=o_sb[:, 1, :])
            else:
                if u == NU - 2:
                    nc.vector.tensor_copy(out=o_sb[:], in_=tiles[0][:])
                else:
                    nc.scalar.copy(out=o_sb[:], in_=tiles[0][:])
                nc.sync.dma_start(out=rows, in_=o_sb[:])

        load_first()
        for u in range(1, AHEAD):
            load(u)
        place_begin(("tabc0", "tabs", "tabc1"))

        quantised = {}
        finished = {}
        for u in range(NU):
            if u < PAIRED:
                quantised.setdefault(u // 2 * 2 + 4, []).append(u)
            elif u > PAIRED:
                quantised.setdefault(u + 2, []).append(u)
            else:
                quantised.setdefault(u + 3, []).append(u)
            if units[u][1] == TT - 1:
                finished.setdefault(u // 2 * 2 + (6 if u < PAIRED else 5) if u < NU - 2 else u + 4, []).append(u)

        for s in range(NU + 4):
            tau = s // PER
            if s % PER == 1 and tau + 1 < TT:
                load_cos(tau + 1)
                load_sin(tau + 1)
            if s + AHEAD < NU:
                load(s + AHEAD)
            if s == 2:
                nc.sync.dma_start(out=v_raw[:], in_=Vf.rearrange("(p j) d -> p j d", j=TT))
            last_of_tau = s % PER == PER - 1 and tau + 1 < TT
            now = quantised.get(s, [])
            end = finished.get(s, [])
            if now:
                quantise(now[0], 2 if now[0] < PAIRED else 1)
            if end:
                scores_quantise(end[0], len(end))
            if s == PER:
                nc.vector.quantize_mx(
                    out=vcodes[:].bitcast(FP8X4), scales=vscales[:], in_=v_grp[:].rearrange("p d j -> p (d j)")
                )
            if s < NU:
                products(s)
            if s == NU - 1:
                quantise(now[1], 1)
                sum_on_vector(s)
            if 0 <= s - 1 < NU:
                rotate_sum(s - 1)
            if last_of_tau:
                place_begin(("tabs", "tabc0", "tabc1"))
                place_sin(tau + 1, 0, CV)
                place_cos(tau + 1, 0, 32)
            for u in now:
                scores(u)
            for u in end:
                values(u)
            if last_of_tau:
                place_cos(tau + 1, 32, NB)
            for u in now:
                scores_out(u)
            for u in end:
                if u == NU - 1:
                    store(u - 1)
                if u != NU - 2:
                    store(u)
            if s == PER - 2:
                nc.scalar.copy(out=v_grp[:], in_=v_raw[:].rearrange("p j d -> p d j"))
